import numpy as np
import ml_dtypes


def mxq(x, axis, fmt="e4m3"):
    dtype, down = {"e4m3": (ml_dtypes.float8_e4m3fn, 7), "e5m2": (ml_dtypes.float8_e5m2, 14)}[fmt]
    v = np.moveaxis(np.asarray(x, np.float32).astype(ml_dtypes.bfloat16).astype(np.float64), axis, -1)
    blocks = v.reshape(v.shape[:-1] + (-1, 32))
    amax = np.abs(blocks).max(-1, keepdims=True)
    byte = np.maximum(np.where(amax > 0, np.frexp(amax)[1] - 1 + 127, 0) - down, 1)
    scale = np.exp2(byte - 127.0)
    codes = (blocks / scale).astype(np.float32).astype(dtype).astype(np.float64)
    return np.moveaxis((codes * scale).reshape(v.shape), -1, axis)


WIDE = False


def mx_kscale(k):
    if not WIDE:
        return np.ones(k)
    levels = np.array([10, -10, 5, -5, 0])
    a = np.random.permutation(np.resize(levels, k // 512 * 4)).reshape(k // 512, 4)
    idx = np.arange(k)
    return np.exp2(a[idx // 512, idx % 128 // 32])


BF16 = ml_dtypes.bfloat16


def bf(x):
    return np.asarray(x, np.float32).astype(BF16)


def f64(x):
    return np.asarray(x).astype(np.float64)


B, T, HS, WS, G, K, CB, CB2, CB3, CB4 = 1, 16, 2, 2, 8, 512, 64, 160, 200, 250
EPS = 1e-3
NV = 5
R = B * T * HS * WS


def bn_apply(v, p):
    gamma, beta, mean, var = p[0], p[1], p[2], p[3]
    return (v - mean) * (gamma / np.sqrt(var + EPS)) + beta


def dwconv_t(v, taps, d):
    vp = np.pad(v, ((0, 0), (d, d), (0, 0), (0, 0), (0, 0), (0, 0)))
    return taps[0] * vp[:, 0:T] + taps[1] * vp[:, d:d + T] + taps[2] * vp[:, 2 * d:2 * d + T]


def setup_inputs():
    s = mx_kscale(K)
    gamma = 1.0 + 0.1 * np.random.standard_normal((NV, G, CB))
    beta = 0.2 * np.random.standard_normal((NV, G, CB))
    mean = 0.04 * np.random.standard_normal((NV, G, CB))
    var = np.random.uniform(0.01, 0.04, (NV, G, CB))
    return {"x": bf(np.random.standard_normal((B, T, HS, WS, G * K)) * np.tile(s, G)),
            "w": bf(np.random.standard_normal((NV, G, K, CB)) * 0.15 / np.sqrt(K) / s[:, None]),
            "b": bf(np.random.standard_normal((NV, G, CB)) * 0.04),
            "dw": bf(np.random.standard_normal((3, 3, G, CB)) * 0.6),
            "bn": bf(np.stack([gamma, beta, mean, var], axis=1))}


def reference(x, w, b, dw, bn):
    b, dw, bn = f64(b), f64(dw), f64(bn)
    xg = f64(x).reshape(R, G, K).transpose(1, 0, 2)
    wg = f64(w).transpose(1, 2, 0, 3).reshape(G, K, NV * CB)
    y = mxq(xg, 2, "e4m3") @ mxq(wg, 1, "e4m3")
    y = y.reshape(G, B, T, HS, WS, NV, CB).transpose(5, 1, 2, 3, 4, 0, 6) + b[:, None, None, None, None]
    outs = [bn_apply(y[0], bn[0])]
    for i, d in enumerate((1, 2, 3)):
        outs.append(bn_apply(dwconv_t(y[1 + i], dw[i], d), bn[1 + i]))
    t5 = np.maximum(y[4], np.concatenate([y[4][:, 1:], y[4][:, -1:]], axis=1))
    outs.append(bn_apply(t5, bn[4]))
    z = np.stack(outs, axis=5)
    z = np.maximum(z.reshape(B, T, HS, WS, G * NV * CB), 0.0)
    z = z.reshape(B, T, HS, WS, G, NV * CB).swapaxes(-1, -2).reshape(B, T, HS, WS, G * NV * CB)
    return z.reshape(B, T // 2, 2, HS, WS, G * NV * CB).max(axis=2)

@@ -1,0 +1,262 @@
+from contextlib import ExitStack
+
+import concourse.mybir as mybir
+from concourse.masks import make_identity
+
+F32 = mybir.dt.float32
+BF16 = mybir.dt.bfloat16
+U32 = mybir.dt.uint32
+U8 = mybir.dt.uint8
+I32 = mybir.dt.int32
+FP8X4 = mybir.dt.float8_e4m3fn_x4
+ALU = mybir.AluOpType
+ACT = mybir.ActivationFunctionType
+
+P = 128
+PACK = 4
+T = 16
+PQ = 4
+R = T * PQ
+G = 8
+K = P * PACK
+CB = 64
+NV = 5
+PAIRS = G // 2
+EPS = 1e-3
+R_OUT = R // 2
+N_PASS = 128
+
+PAIR_COLS = 3 * CB
+W_COLS = NV * PAIRS * PAIR_COLS + CB
+
+BRANCH_ORDER = (4, 1, 2, 3, 0)
+
+FLOPS = 2 * R * K * NV * CB * G
+
+
+def tile_timeception_pa_s_kernel(tc, x, w, b, dw, bn, out):
+    nc = tc.nc
+    with ExitStack() as ctx:
+        keep = ctx.enter_context(tc.tile_pool(name="keep", bufs=1))
+        y_banks = ctx.enter_context(tc.psum_pool(name="y_banks", bufs=1))
+        turn_banks = ctx.enter_context(tc.psum_pool(name="turn_banks", bufs=3))
+
+        x_sb = keep.tile([P, G * K // 2], BF16)
+        nc.sync.dma_start(out=x_sb[:], in_=x.rearrange("n t p q (a c) -> (n t p q a) c", a=2))
+
+        raw = {}
+        for v in BRANCH_ORDER:
+            raw[v] = keep.tile([P, PAIRS, 2, PACK * CB], BF16, name="raw%d" % v)
+            by_parity = w[v].rearrange("(i h) (p j) o -> h p i (j o)", h=2, j=PACK)
+            nc.sync.dma_start(out=raw[v][:, :, 0, :], in_=by_parity[1])
+            nc.sync.dma_start(out=raw[v][:, :, 1, :], in_=by_parity[0])
+
+        par_rows = keep.tile([P, 2, P], BF16)
+        nc.vector.memset(par_rows[:], 0.0)
+        n_bn = NV * 4 * PAIRS
+        n_b = NV * PAIRS
+        n_dw = 3 * 3 * PAIRS
+        nc.scalar.dma_start(out=par_rows[0:n_bn, 0, :], in_=bn.rearrange("v c (i h) o -> (v c i) (h o)", h=2))
+        nc.scalar.dma_start(out=par_rows[n_bn : n_bn + n_b, 0, :], in_=b.rearrange("v (i h) o -> (v i) (h o)", h=2))
+        nc.scalar.dma_start(out=par_rows[0:n_dw, 1, :], in_=dw.rearrange("c k (i h) o -> (c k i) (h o)", h=2))
+
+        ident = keep.tile([P, P], F32)
+        make_identity(nc, ident[:])
+
+        w_codes = keep.tile([P, W_COLS], U32, align_bytes=64)
+        w_scales = keep.tile([P, W_COLS], U8, align_bytes=64)
+        x_codes = keep.tile([P, G * R + R], U32, align_bytes=64)
+        x_scales = keep.tile([P, G * R + R], U8, align_bytes=64)
+        for plane, per_word in ((w_codes, 1), (w_scales, 4)):
+            words = plane[:].bitcast(I32)
+            body = NV * PAIRS * PAIR_COLS // per_word
+            nc.vector.memset(
+                words[:, 0:body].rearrange("p (n c) -> p n c", c=PAIR_COLS // per_word)[:, :, 0 : CB // per_word], 0
+            )
+            nc.vector.memset(words[:, body:], 0)
+        nc.vector.memset(x_codes[:].bitcast(I32)[:, G * R :], 0)
+        nc.vector.memset(x_scales[:].bitcast(I32)[:, G * R // 4 :], 0)
+
+        par_f32 = keep.tile([P, 2, P], F32)
+        nc.vector.tensor_copy(out=par_f32[:], in_=par_rows[:])
+        par_ps = turn_banks.tile([P, 2, P], F32, tag="turn")
+        for s in range(2):
+            nc.tensor.transpose(par_ps[:, s, :], par_f32[:, s, :], ident[:])
+        par = keep.tile([P, 2, P], F32)
+        nc.vector.tensor_copy(out=par[:], in_=par_ps[:])
+        bn_cols = par[:, 0, 0:n_bn].rearrange("p (v c i) -> p v c i", c=4, i=PAIRS)
+        gamma = bn_cols[:, :, 0, :]
+        beta = bn_cols[:, :, 1, :]
+        mean = bn_cols[:, :, 2, :]
+        var = bn_cols[:, :, 3, :]
+        bias = par[:, 0, n_bn : n_bn + n_b].rearrange("p (v i) -> p v i", i=PAIRS)
+        taps = par[:, 1, 0:n_dw].rearrange("p (c k i) -> p c k i", k=3, i=PAIRS)
+
+        gain = keep.tile([P, NV, PAIRS], F32)
+        shift = keep.tile([P, NV, PAIRS], F32)
+        nc.vector.tensor_scalar_add(out=gain[:], in0=var, scalar1=EPS)
+        nc.scalar.sqrt(out=gain[:], in_=gain[:])
+        nc.vector.reciprocal(out=gain[:], in_=gain[:])
+        nc.vector.tensor_mul(out=gain[:], in0=gain[:], in1=gamma)
+        nc.vector.tensor_mul(out=shift[:], in0=gain[:], in1=mean)
+        nc.vector.tensor_sub(out=shift[:], in0=beta, in1=shift[:])
+        offset = keep.tile([P, NV, PAIRS], F32)
+        nc.vector.tensor_mul(out=offset[:], in0=gain[:], in1=bias)
+        nc.vector.tensor_add(out=offset[:], in0=offset[:], in1=shift[:])
+        tap_gain = keep.tile([P, 3, 3, PAIRS], F32)
+        tap_bias = keep.tile([P, 3, 3, PAIRS], F32)
+        conv_offset = keep.tile([P, 3, PAIRS], F32)
+        over_taps = [P, 3, 3, PAIRS]
+        nc.vector.tensor_mul(out=tap_gain[:], in0=taps, in1=gain[:, 1:4, :].unsqueeze(2).to_broadcast(over_taps))
+        nc.vector.tensor_mul(out=tap_bias[:], in0=tap_gain[:], in1=bias[:, 1:4, :].unsqueeze(2).to_broadcast(over_taps))
+        nc.vector.tensor_add(out=conv_offset[:], in0=tap_bias[:, :, 0, :], in1=tap_bias[:, :, 1, :])
+        nc.vector.tensor_add(out=conv_offset[:], in0=conv_offset[:], in1=tap_bias[:, :, 2, :])
+        nc.vector.tensor_add(out=conv_offset[:], in0=conv_offset[:], in1=shift[:, 1:4, :])
+
+        x_words = x_sb[:].bitcast(F32).rearrange("p (gh q u) -> p gh u q", gh=G // 2, u=2)
+        x_grouped = keep.tile([P, G * R * PACK], BF16, align_bytes=64)
+        x_grouped_words = x_grouped[:].bitcast(F32).rearrange(
+            "p (a bk gl r u) -> p a bk gl r u", a=2, bk=2, gl=2, u=2
+        )
+        for bk in range(2):
+            x_ps = turn_banks.tile([P, 2, 2, P], F32, tag="turn")
+            for gl in range(2):
+                for u in range(2):
+                    nc.tensor.transpose(x_ps[:, gl, u, :], x_words[:, 2 * bk + gl, u, :], ident[:])
+            by_half = x_ps[:].rearrange("p gl u (r a) -> p a gl r u", a=2)
+            for a in range(2):
+                if bk == 0:
+                    nc.vector.tensor_copy(out=x_grouped_words[:, a, bk], in_=by_half[:, a])
+                else:
+                    nc.scalar.copy(out=x_grouped_words[:, a, bk], in_=by_half[:, a])
+        nc.vector.quantize_mx(
+            out=x_codes[:, 0 : G * R].bitcast(FP8X4), scales=x_scales[:, 0 : G * R], in_=x_grouped[:]
+        )
+
+        z = keep.tile([P, PAIRS, NV, R], F32)
+        z_max = keep.tile([P, PAIRS, NV, R_OUT], F32)
+
+        def matmuls(v, slot):
+            grouped = keep.tile([P, PAIRS, 2, CB * PACK], BF16, name="grouped%d" % v, align_bytes=64)
+            half = PAIRS // 2
+            nc.vector.tensor_copy(
+                out=grouped[:, 0:half].rearrange("p i h (c f j) -> p (i h) c j f", f=4, j=PACK),
+                in_=raw[v][:, 0:half].rearrange("p i h (j c f) -> p (i h) c j f", f=4, j=PACK),
+            )
+            nc.scalar.copy(
+                out=grouped[:, half:PAIRS].rearrange("p i h (o j) -> p (i h) o j", j=PACK),
+                in_=raw[v][:, half:PAIRS].rearrange("p i h (j o) -> p (i h) o j", j=PACK),
+            )
+            y = y_banks.tile([P, PAIRS, N_PASS], F32, name="y%d" % v)
+            for i in range(PAIRS):
+                z_col = (slot * PAIRS + i) * PAIR_COLS
+                ab_cols = slice(z_col + CB, z_col + 3 * CB)
+                nc.vector.quantize_mx(
+                    out=w_codes[:, ab_cols].bitcast(FP8X4),
+                    scales=w_scales[:, ab_cols],
+                    in_=grouped[:, i].rearrange("p h c -> p (h c)"),
+                )
+                for first, g, col in ((True, 2 * i + 1, z_col), (False, 2 * i, z_col + 2 * CB)):
+                    nc.tensor.matmul_mx(
+                        out=y[:, i, :],
+                        lhsT=w_codes[:, col : col + P].bitcast(FP8X4),
+                        lhsT_scale=w_scales[:, col : col + P],
+                        rhs=x_codes[:, g * R : g * R + N_PASS].bitcast(FP8X4),
+                        rhs_scale=x_scales[:, g * R : g * R + N_PASS],
+                        start=first,
+                        stop=not first,
+                    )
+            return y
+
+        def affine(v, src):
+            for i in range(PAIRS):
+                nc.scalar.activation(
+                    out=z[:, i, v, :],
+                    in_=src[:, i, 0:R],
+                    func=ACT.Identity,
+                    scale=gain[:, v, i : i + 1],
+                    bias=offset[:, v, i : i + 1],
+                )
+
+        def conv(v, y):
+            c = v - 1
+            edge = v * PQ
+            for i in range(PAIRS):
+                nc.vector.tensor_scalar(
+                    out=z[:, i, v, :],
+                    in0=y[:, i, 0:R],
+                    scalar1=tap_gain[:, c, 1, i : i + 1],
+                    scalar2=conv_offset[:, c, i : i + 1],
+                    op0=ALU.mult,
+                    op1=ALU.add,
+                )
+            for k, dst, src in ((0, slice(edge, R), slice(0, R - edge)), (2, slice(0, R - edge), slice(edge, R))):
+                for i in range(PAIRS):
+                    nc.vector.scalar_tensor_tensor(
+                        out=z[:, i, v, dst],
+                        in0=y[:, i, src],
+                        scalar=tap_gain[:, c, k, i : i + 1],
+                        in1=z[:, i, v, dst],
+                        op0=ALU.mult,
+                        op1=ALU.add,
+                    )
+            for k, cols in ((0, slice(0, edge)), (2, slice(R - edge, R))):
+                nc.vector.tensor_sub(
+                    out=z[:, :, v, cols],
+                    in0=z[:, :, v, cols],
+                    in1=tap_bias[:, c, k, :].unsqueeze(2).to_broadcast([P, PAIRS, edge]),
+                )
+
+        def max_next(y):
+            y_sb = keep.tile([P, PAIRS, R + PQ], F32)
+            nc.scalar.copy(out=y_sb[:, :, 0:R], in_=y[:, :, 0:R])
+            nc.scalar.copy(out=y_sb[:, :, R : R + PQ], in_=y[:, :, R - PQ : R])
+            u = keep.tile([P, PAIRS, R], F32)
+            nc.vector.tensor_max(out=u[:], in0=y_sb[:, :, 0:R], in1=y_sb[:, :, PQ : R + PQ])
+            return u
+
+        def max_pairs_of_steps(v):
+            steps = z[:, :, v, :].rearrange("p i (t two q) -> p i t two q", two=2, q=PQ)
+            nc.vector.tensor_max(
+                out=z_max[:, :, v, :].rearrange("p i (t q) -> p i t q", q=PQ),
+                in0=steps[:, :, :, 0, :],
+                in1=steps[:, :, :, 1, :],
+            )
+
+        out_rows = out.rearrange("n t p q c -> (n t p q) c")
+        z_cols = z_max[:].rearrange("p i v r -> p i (v r)")
+
+        def shuffle_and_store(first_branch, used):
+            turned = turn_banks.tile([P, G * CB], F32, tag="turn")
+            for i in range(PAIRS):
+                nc.tensor.transpose(
+                    turned[:, i * P : (i + 1) * P],
+                    z_cols[:, i, first_branch * R_OUT : first_branch * R_OUT + P],
+                    ident[:],
+                )
+            rows = slice(used[0] * R_OUT, (used[-1] + 1) * R_OUT)
+            shuffled = keep.tile([P, CB * G], F32, name="shuffled%d" % first_branch)
+            nc.scalar.activation(
+                out=shuffled[rows, :].rearrange("p (o g) -> p o g", g=G),
+                in_=turned[rows, :].rearrange("p (g o) -> p o g", o=CB),
+                func=ACT.Relu,
+            )
+            for s in used:
+                v = first_branch + s
+                nc.sync.dma_start(
+                    out=out_rows[:, v * CB * G : (v + 1) * CB * G],
+                    in_=shuffled[s * R_OUT : (s + 1) * R_OUT, :],
+                )
+
+        for slot, v in enumerate(BRANCH_ORDER):
+            y = matmuls(v, slot)
+            if v == 0:
+                affine(v, y)
+            elif v == 4:
+                affine(v, max_next(y))
+            else:
+                conv(v, y)
+            max_pairs_of_steps(v)
+            if v == 3:
+                shuffle_and_store(1, (0, 1, 2, 3))
+        shuffle_and_store(0, (0,))

@@ -26,10 +26,15 @@ EPS = 1e-3
 R_OUT = R // 2
 N_PASS = 128
 
-PAIR_COLS = 3 * CB
-W_COLS = NV * PAIRS * PAIR_COLS + CB
+UNIT_GROUPS = 4
+UNITS = NV * G // UNIT_GROUPS
 
-BRANCH_ORDER = (4, 1, 2, 3, 0)
+PAIR_COLS = 3 * CB
+W_COLS = NV * PAIRS * PAIR_COLS
+
+V_CHANNELS = 16
+
+BRANCH_ORDER = (1, 2, 3, 4, 0)
 
 FLOPS = 2 * R * K * NV * CB * G
 
@@ -40,153 +45,180 @@ def tile_timeception_pa_s_kernel(tc, x, w, b, dw, bn, out):
         keep = ctx.enter_context(tc.tile_pool(name="keep", bufs=1))
         y_banks = ctx.enter_context(tc.psum_pool(name="y_banks", bufs=1))
         turn_banks = ctx.enter_context(tc.psum_pool(name="turn_banks", bufs=3))
+        ctx.enter_context(tc.manual_schedule())
 
-        x_sb = keep.tile([P, G * K // 2], BF16)
-        nc.sync.dma_start(out=x_sb[:], in_=x.rearrange("n t p q (a c) -> (n t p q a) c", a=2))
-
-        raw = {}
-        for v in BRANCH_ORDER:
-            raw[v] = keep.tile([P, PAIRS, 2, PACK * CB], BF16, name="raw%d" % v)
-            by_parity = w[v].rearrange("(i h) (p j) o -> h p i (j o)", h=2, j=PACK)
-            nc.sync.dma_start(out=raw[v][:, :, 0, :], in_=by_parity[1])
-            nc.sync.dma_start(out=raw[v][:, :, 1, :], in_=by_parity[0])
-
-        par_rows = keep.tile([P, 2, P], BF16)
-        nc.vector.memset(par_rows[:], 0.0)
         n_bn = NV * 4 * PAIRS
         n_b = NV * PAIRS
         n_dw = 3 * 3 * PAIRS
+        par_rows = keep.tile([P, 2, P], BF16)
+        nc.gpsimd.memset(par_rows[:], 0.0)
         nc.scalar.dma_start(out=par_rows[0:n_bn, 0, :], in_=bn.rearrange("v c (i h) o -> (v c i) (h o)", h=2))
         nc.scalar.dma_start(out=par_rows[n_bn : n_bn + n_b, 0, :], in_=b.rearrange("v (i h) o -> (v i) (h o)", h=2))
         nc.scalar.dma_start(out=par_rows[0:n_dw, 1, :], in_=dw.rearrange("c k (i h) o -> (c k i) (h o)", h=2))
 
+        x_sb = keep.tile([P, G * K // 2], BF16)
+        nc.sync.dma_start(out=x_sb[:], in_=x.rearrange("n t p q (a c) -> (n t p q a) c", a=2))
+        raw = []
+        for unit in range(UNITS):
+            v = BRANCH_ORDER[unit // 2]
+            g0 = (unit % 2) * UNIT_GROUPS
+            raw.append(keep.tile([P, UNIT_GROUPS, PACK * CB], BF16, name="raw%d" % unit))
+            nc.sync.dma_start(
+                out=raw[unit][:], in_=w[v, g0 : g0 + UNIT_GROUPS].rearrange("g (p j) o -> p g (j o)", j=PACK)
+            )
+
+        warm = keep.tile([P, 1], F32)
+        nc.gpsimd.memset(warm[:], 1.0)
+        nc.scalar.activation(out=warm[:], in_=warm[:], func=ACT.Abs_reciprocal_sqrt)
         ident = keep.tile([P, P], F32)
         make_identity(nc, ident[:])
+        ident_bf = keep.tile([P, P], BF16)
+        make_identity(nc, ident_bf[:])
 
         w_codes = keep.tile([P, W_COLS], U32, align_bytes=64)
         w_scales = keep.tile([P, W_COLS], U8, align_bytes=64)
         x_codes = keep.tile([P, G * R + R], U32, align_bytes=64)
         x_scales = keep.tile([P, G * R + R], U8, align_bytes=64)
-        for plane, per_word in ((w_codes, 1), (w_scales, 4)):
-            words = plane[:].bitcast(I32)
-            body = NV * PAIRS * PAIR_COLS // per_word
-            nc.vector.memset(
-                words[:, 0:body].rearrange("p (n c) -> p n c", c=PAIR_COLS // per_word)[:, :, 0 : CB // per_word], 0
-            )
-            nc.vector.memset(words[:, body:], 0)
+        nc.vector.memset(w_codes[:].bitcast(I32).rearrange("p (n c) -> p n c", c=PAIR_COLS)[:, :, CB : 2 * CB], 0)
+        nc.vector.memset(
+            w_scales[:].bitcast(I32).rearrange("p (n c) -> p n c", c=PAIR_COLS // 4)[:, :, CB // 4 : CB // 2], 0
+        )
         nc.vector.memset(x_codes[:].bitcast(I32)[:, G * R :], 0)
         nc.vector.memset(x_scales[:].bitcast(I32)[:, G * R // 4 :], 0)
-
-        par_f32 = keep.tile([P, 2, P], F32)
-        nc.vector.tensor_copy(out=par_f32[:], in_=par_rows[:])
-        par_ps = turn_banks.tile([P, 2, P], F32, tag="turn")
-        for s in range(2):
-            nc.tensor.transpose(par_ps[:, s, :], par_f32[:, s, :], ident[:])
-        par = keep.tile([P, 2, P], F32)
-        nc.vector.tensor_copy(out=par[:], in_=par_ps[:])
-        bn_cols = par[:, 0, 0:n_bn].rearrange("p (v c i) -> p v c i", c=4, i=PAIRS)
-        gamma = bn_cols[:, :, 0, :]
-        beta = bn_cols[:, :, 1, :]
-        mean = bn_cols[:, :, 2, :]
-        var = bn_cols[:, :, 3, :]
-        bias = par[:, 0, n_bn : n_bn + n_b].rearrange("p (v i) -> p v i", i=PAIRS)
-        taps = par[:, 1, 0:n_dw].rearrange("p (c k i) -> p c k i", k=3, i=PAIRS)
-
-        gain = keep.tile([P, NV, PAIRS], F32)
-        shift = keep.tile([P, NV, PAIRS], F32)
-        nc.vector.tensor_scalar_add(out=gain[:], in0=var, scalar1=EPS)
-        nc.scalar.sqrt(out=gain[:], in_=gain[:])
-        nc.vector.reciprocal(out=gain[:], in_=gain[:])
-        nc.vector.tensor_mul(out=gain[:], in0=gain[:], in1=gamma)
-        nc.vector.tensor_mul(out=shift[:], in0=gain[:], in1=mean)
-        nc.vector.tensor_sub(out=shift[:], in0=beta, in1=shift[:])
-        offset = keep.tile([P, NV, PAIRS], F32)
-        nc.vector.tensor_mul(out=offset[:], in0=gain[:], in1=bias)
-        nc.vector.tensor_add(out=offset[:], in0=offset[:], in1=shift[:])
-        tap_gain = keep.tile([P, 3, 3, PAIRS], F32)
-        tap_bias = keep.tile([P, 3, 3, PAIRS], F32)
-        conv_offset = keep.tile([P, 3, PAIRS], F32)
-        over_taps = [P, 3, 3, PAIRS]
-        nc.vector.tensor_mul(out=tap_gain[:], in0=taps, in1=gain[:, 1:4, :].unsqueeze(2).to_broadcast(over_taps))
-        nc.vector.tensor_mul(out=tap_bias[:], in0=tap_gain[:], in1=bias[:, 1:4, :].unsqueeze(2).to_broadcast(over_taps))
-        nc.vector.tensor_add(out=conv_offset[:], in0=tap_bias[:, :, 0, :], in1=tap_bias[:, :, 1, :])
-        nc.vector.tensor_add(out=conv_offset[:], in0=conv_offset[:], in1=tap_bias[:, :, 2, :])
-        nc.vector.tensor_add(out=conv_offset[:], in0=conv_offset[:], in1=shift[:, 1:4, :])
 
         x_words = x_sb[:].bitcast(F32).rearrange("p (gh q u) -> p gh u q", gh=G // 2, u=2)
         x_grouped = keep.tile([P, G * R * PACK], BF16, align_bytes=64)
         x_grouped_words = x_grouped[:].bitcast(F32).rearrange(
             "p (a bk gl r u) -> p a bk gl r u", a=2, bk=2, gl=2, u=2
         )
-        for bk in range(2):
+
+        def turn_x(bk):
             x_ps = turn_banks.tile([P, 2, 2, P], F32, tag="turn")
             for gl in range(2):
                 for u in range(2):
                     nc.tensor.transpose(x_ps[:, gl, u, :], x_words[:, 2 * bk + gl, u, :], ident[:])
+            return x_ps
+
+        def copy_x(bk, x_ps):
             by_half = x_ps[:].rearrange("p gl u (r a) -> p a gl r u", a=2)
             for a in range(2):
                 if bk == 0:
                     nc.vector.tensor_copy(out=x_grouped_words[:, a, bk], in_=by_half[:, a])
                 else:
                     nc.scalar.copy(out=x_grouped_words[:, a, bk], in_=by_half[:, a])
-        nc.vector.quantize_mx(
-            out=x_codes[:, 0 : G * R].bitcast(FP8X4), scales=x_scales[:, 0 : G * R], in_=x_grouped[:]
-        )
+
+        par = keep.tile([P, n_bn + n_b], F32)
+        bn_cols = par[:, 0:n_bn].rearrange("p (v c i) -> p v c i", c=4, i=PAIRS)
+        gamma = bn_cols[:, :, 0, :]
+        beta = bn_cols[:, :, 1, :]
+        mean = bn_cols[:, :, 2, :]
+        bias = par[:, n_bn : n_bn + n_b].rearrange("p (v i) -> p v i", i=PAIRS)
+        taps = keep.tile([P, NV, 3, PAIRS], F32)
+        nc.gpsimd.memset(taps[:], 0.0)
+        nc.gpsimd.memset(taps[:, 0 : NV : NV - 1, 1, :], 1.0)
+        gain = keep.tile([P, NV, PAIRS], F32)
+        shift = keep.tile([P, NV, PAIRS], F32)
+        offset = keep.tile([P, NV, PAIRS], F32)
+        tap_gain = keep.tile([P, NV, 3, PAIRS], F32)
+        tap_bias = keep.tile([P, NV, 3, PAIRS], F32)
+
+        def turn_parameters():
+            par_ps = turn_banks.tile([P, 2, P], BF16, tag="turn")
+            for s in range(2):
+                nc.tensor.transpose(par_ps[:, s, :], par_rows[:, s, :], ident_bf[:])
+            return par_ps
+
+        def unpack_parameters(par_ps):
+            nc.vector.tensor_copy(out=par[:], in_=par_ps[:, 0, 0 : n_bn + n_b])
+            nc.vector.tensor_copy(out=taps[:, 1:4].rearrange("p c k i -> p (c k i)"), in_=par_ps[:, 1, 0:n_dw])
+            nc.vector.tensor_scalar_add(out=gain[:], in0=bn_cols[:, :, 3, :], scalar1=EPS)
+            nc.scalar.activation(out=gain[:], in_=gain[:], func=ACT.Abs_reciprocal_sqrt)
+
+        def fold_parameters():
+            over_taps = [P, NV, 3, PAIRS]
+            nc.vector.tensor_mul(out=gain[:], in0=gain[:], in1=gamma)
+            nc.vector.tensor_mul(out=tap_gain[:], in0=taps[:], in1=gain[:].unsqueeze(2).to_broadcast(over_taps))
+            nc.vector.tensor_mul(out=shift[:], in0=gain[:], in1=mean)
+            nc.vector.tensor_mul(out=tap_bias[:], in0=tap_gain[:], in1=bias.unsqueeze(2).to_broadcast(over_taps))
+            nc.vector.tensor_sub(out=shift[:], in0=beta, in1=shift[:])
+            nc.vector.tensor_reduce(
+                out=offset[:], in_=tap_bias[:].rearrange("p v k i -> p v i k"), axis=mybir.AxisListType.X, op=ALU.add
+            )
+            nc.vector.tensor_add(out=offset[:], in0=offset[:], in1=shift[:])
+
+        grouped = [
+            keep.tile([P, UNIT_GROUPS, CB * PACK], BF16, name="grouped%d" % unit, align_bytes=64)
+            for unit in range(UNITS)
+        ]
+        y = {}
+
+        def regroup(unit):
+            runs = V_CHANNELS // 4
+            nc.vector.tensor_copy(
+                out=grouped[unit][:].rearrange("p g (c f j) -> p g c j f", f=4, j=PACK)[:, :, 0:runs],
+                in_=raw[unit][:].rearrange("p g (j c f) -> p g c j f", f=4, j=PACK)[:, :, 0:runs],
+            )
+            nc.scalar.copy(
+                out=grouped[unit][:].rearrange("p g (o j) -> p g o j", j=PACK)[:, :, V_CHANNELS:CB],
+                in_=raw[unit][:].rearrange("p g (j o) -> p g o j", j=PACK)[:, :, V_CHANNELS:CB],
+            )
+
+        def quantise_and_multiply(unit):
+            slot = unit // 2
+            v = BRANCH_ORDER[slot]
+            if unit % 2 == 0:
+                y[v] = y_banks.tile([P, PAIRS, N_PASS], F32, name="y%d" % v)
+            for gl in range(UNIT_GROUPS):
+                g = (unit % 2) * UNIT_GROUPS + gl
+                col = (slot * PAIRS + g // 2) * PAIR_COLS + (g % 2) * 2 * CB
+                nc.vector.quantize_mx(
+                    out=w_codes[:, col : col + CB].bitcast(FP8X4),
+                    scales=w_scales[:, col : col + CB],
+                    in_=grouped[unit][:, gl, :],
+                )
+            for gl in range(UNIT_GROUPS):
+                g = (unit % 2) * UNIT_GROUPS + gl
+                col = (slot * PAIRS + g // 2) * PAIR_COLS + (g % 2) * CB
+                nc.tensor.matmul_mx(
+                    out=y[v][:, g // 2, :],
+                    lhsT=w_codes[:, col : col + P].bitcast(FP8X4),
+                    lhsT_scale=w_scales[:, col : col + P],
+                    rhs=x_codes[:, g * R : g * R + N_PASS].bitcast(FP8X4),
+                    rhs_scale=x_scales[:, g * R : g * R + N_PASS],
+                    start=(g % 2 == 0),
+                    stop=(g % 2 == 1),
+                )
 
         z = keep.tile([P, PAIRS, NV, R], F32)
         z_max = keep.tile([P, PAIRS, NV, R_OUT], F32)
+        y4_sb = keep.tile([P, PAIRS, R + PQ], F32)
+        u4 = keep.tile([P, PAIRS, R], F32)
 
-        def matmuls(v, slot):
-            grouped = keep.tile([P, PAIRS, 2, CB * PACK], BF16, name="grouped%d" % v, align_bytes=64)
-            half = PAIRS // 2
-            nc.vector.tensor_copy(
-                out=grouped[:, 0:half].rearrange("p i h (c f j) -> p (i h) c j f", f=4, j=PACK),
-                in_=raw[v][:, 0:half].rearrange("p i h (j c f) -> p (i h) c j f", f=4, j=PACK),
-            )
-            nc.scalar.copy(
-                out=grouped[:, half:PAIRS].rearrange("p i h (o j) -> p (i h) o j", j=PACK),
-                in_=raw[v][:, half:PAIRS].rearrange("p i h (j o) -> p (i h) o j", j=PACK),
-            )
-            y = y_banks.tile([P, PAIRS, N_PASS], F32, name="y%d" % v)
-            for i in range(PAIRS):
-                z_col = (slot * PAIRS + i) * PAIR_COLS
-                ab_cols = slice(z_col + CB, z_col + 3 * CB)
-                nc.vector.quantize_mx(
-                    out=w_codes[:, ab_cols].bitcast(FP8X4),
-                    scales=w_scales[:, ab_cols],
-                    in_=grouped[:, i].rearrange("p h c -> p (h c)"),
-                )
-                for first, g, col in ((True, 2 * i + 1, z_col), (False, 2 * i, z_col + 2 * CB)):
-                    nc.tensor.matmul_mx(
-                        out=y[:, i, :],
-                        lhsT=w_codes[:, col : col + P].bitcast(FP8X4),
-                        lhsT_scale=w_scales[:, col : col + P],
-                        rhs=x_codes[:, g * R : g * R + N_PASS].bitcast(FP8X4),
-                        rhs_scale=x_scales[:, g * R : g * R + N_PASS],
-                        start=first,
-                        stop=not first,
+        def epilogue_on_scalar(v):
+            if v == 0:
+                for i in range(PAIRS):
+                    nc.scalar.activation(
+                        out=z[:, i, v, :],
+                        in_=y[v][:, i, 0:R],
+                        func=ACT.Identity,
+                        scale=tap_gain[:, v, 1, i : i + 1],
+                        bias=offset[:, v, i : i + 1],
                     )
-            return y
+            if v == 4:
+                nc.scalar.copy(out=y4_sb[:, :, 0:R], in_=y[v][:, :, 0:R])
+                nc.scalar.copy(out=y4_sb[:, :, R : R + PQ], in_=y[v][:, :, R - PQ : R])
 
-        def affine(v, src):
-            for i in range(PAIRS):
-                nc.scalar.activation(
-                    out=z[:, i, v, :],
-                    in_=src[:, i, 0:R],
-                    func=ACT.Identity,
-                    scale=gain[:, v, i : i + 1],
-                    bias=offset[:, v, i : i + 1],
-                )
-
-        def conv(v, y):
-            c = v - 1
+        def taps_or_max(v):
+            if v == 4:
+                nc.vector.tensor_max(out=u4[:], in0=y4_sb[:, :, 0:R], in1=y4_sb[:, :, PQ : R + PQ])
+                return
             edge = v * PQ
             for i in range(PAIRS):
                 nc.vector.tensor_scalar(
                     out=z[:, i, v, :],
-                    in0=y[:, i, 0:R],
-                    scalar1=tap_gain[:, c, 1, i : i + 1],
-                    scalar2=conv_offset[:, c, i : i + 1],
+                    in0=y[v][:, i, 0:R],
+                    scalar1=tap_gain[:, v, 1, i : i + 1],
+                    scalar2=offset[:, v, i : i + 1],
                     op0=ALU.mult,
                     op1=ALU.add,
                 )
@@ -194,28 +226,34 @@ def tile_timeception_pa_s_kernel(tc, x, w, b, dw, bn, out):
                 for i in range(PAIRS):
                     nc.vector.scalar_tensor_tensor(
                         out=z[:, i, v, dst],
-                        in0=y[:, i, src],
-                        scalar=tap_gain[:, c, k, i : i + 1],
+                        in0=y[v][:, i, src],
+                        scalar=tap_gain[:, v, k, i : i + 1],
                         in1=z[:, i, v, dst],
                         op0=ALU.mult,
                         op1=ALU.add,
                     )
+
+        def edges_or_affine(v):
+            if v == 4:
+                for i in range(PAIRS):
+                    nc.vector.tensor_scalar(
+                        out=z[:, i, v, :],
+                        in0=u4[:, i, :],
+                        scalar1=tap_gain[:, v, 1, i : i + 1],
+                        scalar2=offset[:, v, i : i + 1],
+                        op0=ALU.mult,
+                        op1=ALU.add,
+                    )
+                return
+            edge = v * PQ
             for k, cols in ((0, slice(0, edge)), (2, slice(R - edge, R))):
                 nc.vector.tensor_sub(
                     out=z[:, :, v, cols],
                     in0=z[:, :, v, cols],
-                    in1=tap_bias[:, c, k, :].unsqueeze(2).to_broadcast([P, PAIRS, edge]),
+                    in1=tap_bias[:, v, k, :].unsqueeze(2).to_broadcast([P, PAIRS, edge]),
                 )
 
-        def max_next(y):
-            y_sb = keep.tile([P, PAIRS, R + PQ], F32)
-            nc.scalar.copy(out=y_sb[:, :, 0:R], in_=y[:, :, 0:R])
-            nc.scalar.copy(out=y_sb[:, :, R : R + PQ], in_=y[:, :, R - PQ : R])
-            u = keep.tile([P, PAIRS, R], F32)
-            nc.vector.tensor_max(out=u[:], in0=y_sb[:, :, 0:R], in1=y_sb[:, :, PQ : R + PQ])
-            return u
-
-        def max_pairs_of_steps(v):
+        def max_of_step_pairs(v):
             steps = z[:, :, v, :].rearrange("p i (t two q) -> p i t two q", two=2, q=PQ)
             nc.vector.tensor_max(
                 out=z_max[:, :, v, :].rearrange("p i (t q) -> p i t q", q=PQ),
@@ -226,7 +264,7 @@ def tile_timeception_pa_s_kernel(tc, x, w, b, dw, bn, out):
         out_rows = out.rearrange("n t p q c -> (n t p q) c")
         z_cols = z_max[:].rearrange("p i v r -> p i (v r)")
 
-        def shuffle_and_store(first_branch, used):
+        def turn_branches(first_branch):
             turned = turn_banks.tile([P, G * CB], F32, tag="turn")
             for i in range(PAIRS):
                 nc.tensor.transpose(
@@ -234,29 +272,51 @@ def tile_timeception_pa_s_kernel(tc, x, w, b, dw, bn, out):
                     z_cols[:, i, first_branch * R_OUT : first_branch * R_OUT + P],
                     ident[:],
                 )
-            rows = slice(used[0] * R_OUT, (used[-1] + 1) * R_OUT)
+            return turned
+
+        def relu_shuffle_store(turned, first_branch, n_used, on_vector):
+            rows = slice(0, n_used * R_OUT)
             shuffled = keep.tile([P, CB * G], F32, name="shuffled%d" % first_branch)
-            nc.scalar.activation(
-                out=shuffled[rows, :].rearrange("p (o g) -> p o g", g=G),
-                in_=turned[rows, :].rearrange("p (g o) -> p o g", o=CB),
-                func=ACT.Relu,
-            )
-            for s in used:
+            dst = shuffled[rows, :].rearrange("p (o g) -> p o g", g=G)
+            src = turned[rows, :].rearrange("p (g o) -> p o g", o=CB)
+            if on_vector:
+                nc.vector.tensor_scalar_max(out=dst, in0=src, scalar1=0.0)
+            else:
+                nc.scalar.activation(out=dst, in_=src, func=ACT.Relu)
+            for s in range(n_used):
                 v = first_branch + s
                 nc.sync.dma_start(
                     out=out_rows[:, v * CB * G : (v + 1) * CB * G],
                     in_=shuffled[s * R_OUT : (s + 1) * R_OUT, :],
                 )
 
-        for slot, v in enumerate(BRANCH_ORDER):
-            y = matmuls(v, slot)
-            if v == 0:
-                affine(v, y)
-            elif v == 4:
-                affine(v, max_next(y))
-            else:
-                conv(v, y)
-            max_pairs_of_steps(v)
-            if v == 3:
-                shuffle_and_store(1, (0, 1, 2, 3))
-        shuffle_and_store(0, (0,))
+        x_ps0 = turn_x(0)
+        x_ps1 = turn_x(1)
+        par_ps = turn_parameters()
+        regroup(0)
+        copy_x(0, x_ps0)
+        copy_x(1, x_ps1)
+        unpack_parameters(par_ps)
+        regroup(1)
+        nc.vector.quantize_mx(
+            out=x_codes[:, 0 : G * R].bitcast(FP8X4), scales=x_scales[:, 0 : G * R], in_=x_grouped[:]
+        )
+        fold_parameters()
+        for unit in range(UNITS):
+            finished = BRANCH_ORDER[(unit - 3) // 2] if unit % 2 == 1 and unit >= 3 else None
+            if finished is not None:
+                epilogue_on_scalar(finished)
+                taps_or_max(finished)
+            quantise_and_multiply(unit)
+            if finished is not None:
+                edges_or_affine(finished)
+            if unit + 2 < UNITS:
+                regroup(unit + 2)
+            if finished is not None:
+                max_of_step_pairs(finished)
+        epilogue_on_scalar(0)
+        turned_1234 = turn_branches(1)
+        max_of_step_pairs(0)
+        relu_shuffle_store(turned_1234, 1, 4, True)
+        turned_0123 = turn_branches(0)
+        relu_shuffle_store(turned_0123, 0, 1, False)

@@ -30,9 +30,7 @@ UNIT_GROUPS = 4
 UNITS = NV * G // UNIT_GROUPS
 
 PAIR_COLS = 3 * CB
-W_COLS = NV * PAIRS * PAIR_COLS
-
-V_CHANNELS = 16
+W_COLS = NV * PAIRS * PAIR_COLS + CB
 
 BRANCH_ORDER = (1, 2, 3, 4, 0)
 
@@ -79,10 +77,13 @@ def tile_timeception_pa_s_kernel(tc, x, w, b, dw, bn, out):
         w_scales = keep.tile([P, W_COLS], U8, align_bytes=64)
         x_codes = keep.tile([P, G * R + R], U32, align_bytes=64)
         x_scales = keep.tile([P, G * R + R], U8, align_bytes=64)
-        nc.vector.memset(w_codes[:].bitcast(I32).rearrange("p (n c) -> p n c", c=PAIR_COLS)[:, :, CB : 2 * CB], 0)
-        nc.vector.memset(
-            w_scales[:].bitcast(I32).rearrange("p (n c) -> p n c", c=PAIR_COLS // 4)[:, :, CB // 4 : CB // 2], 0
-        )
+        for plane, per_word in ((w_codes, 1), (w_scales, 4)):
+            words = plane[:].bitcast(I32)
+            body = (W_COLS - CB) // per_word
+            nc.vector.memset(
+                words[:, 0:body].rearrange("p (n c) -> p n c", c=PAIR_COLS // per_word)[:, :, 0 : CB // per_word], 0
+            )
+            nc.vector.memset(words[:, body:], 0)
         nc.vector.memset(x_codes[:].bitcast(I32)[:, G * R :], 0)
         nc.vector.memset(x_scales[:].bitcast(I32)[:, G * R // 4 :], 0)
 
@@ -102,25 +103,23 @@ def tile_timeception_pa_s_kernel(tc, x, w, b, dw, bn, out):
         def copy_x(bk, x_ps):
             by_half = x_ps[:].rearrange("p gl u (r a) -> p a gl r u", a=2)
             for a in range(2):
-                if bk == 0:
-                    nc.vector.tensor_copy(out=x_grouped_words[:, a, bk], in_=by_half[:, a])
-                else:
-                    nc.scalar.copy(out=x_grouped_words[:, a, bk], in_=by_half[:, a])
+                nc.scalar.copy(out=x_grouped_words[:, a, bk], in_=by_half[:, a])
 
         par = keep.tile([P, n_bn + n_b], F32)
         bn_cols = par[:, 0:n_bn].rearrange("p (v c i) -> p v c i", c=4, i=PAIRS)
         gamma = bn_cols[:, :, 0, :]
         beta = bn_cols[:, :, 1, :]
         mean = bn_cols[:, :, 2, :]
+        var = bn_cols[:, :, 3, :]
         bias = par[:, n_bn : n_bn + n_b].rearrange("p (v i) -> p v i", i=PAIRS)
         taps = keep.tile([P, NV, 3, PAIRS], F32)
         nc.gpsimd.memset(taps[:], 0.0)
         nc.gpsimd.memset(taps[:, 0 : NV : NV - 1, 1, :], 1.0)
         gain = keep.tile([P, NV, PAIRS], F32)
-        shift = keep.tile([P, NV, PAIRS], F32)
         offset = keep.tile([P, NV, PAIRS], F32)
         tap_gain = keep.tile([P, NV, 3, PAIRS], F32)
         tap_bias = keep.tile([P, NV, 3, PAIRS], F32)
+        over_taps = [P, NV, 3, PAIRS]
 
         def turn_parameters():
             par_ps = turn_banks.tile([P, 2, P], BF16, tag="turn")
@@ -131,20 +130,21 @@ def tile_timeception_pa_s_kernel(tc, x, w, b, dw, bn, out):
         def unpack_parameters(par_ps):
             nc.vector.tensor_copy(out=par[:], in_=par_ps[:, 0, 0 : n_bn + n_b])
             nc.vector.tensor_copy(out=taps[:, 1:4].rearrange("p c k i -> p (c k i)"), in_=par_ps[:, 1, 0:n_dw])
-            nc.vector.tensor_scalar_add(out=gain[:], in0=bn_cols[:, :, 3, :], scalar1=EPS)
-            nc.scalar.activation(out=gain[:], in_=gain[:], func=ACT.Abs_reciprocal_sqrt)
+            nc.vector.tensor_scalar_add(out=gain[:], in0=var, scalar1=EPS)
 
-        def fold_parameters():
-            over_taps = [P, NV, 3, PAIRS]
+        def fold_without_gain():
+            nc.gpsimd.tensor_add(out=offset[:], in0=taps[:, :, 0, :], in1=taps[:, :, 1, :])
+            nc.gpsimd.tensor_mul(out=tap_bias[:], in0=taps[:], in1=bias.unsqueeze(2).to_broadcast(over_taps))
+            nc.gpsimd.tensor_add(out=offset[:], in0=offset[:], in1=taps[:, :, 2, :])
+            nc.gpsimd.tensor_mul(out=offset[:], in0=offset[:], in1=bias)
+            nc.gpsimd.tensor_sub(out=offset[:], in0=offset[:], in1=mean)
+
+        def fold_with_gain():
             nc.vector.tensor_mul(out=gain[:], in0=gain[:], in1=gamma)
             nc.vector.tensor_mul(out=tap_gain[:], in0=taps[:], in1=gain[:].unsqueeze(2).to_broadcast(over_taps))
-            nc.vector.tensor_mul(out=shift[:], in0=gain[:], in1=mean)
-            nc.vector.tensor_mul(out=tap_bias[:], in0=tap_gain[:], in1=bias.unsqueeze(2).to_broadcast(over_taps))
-            nc.vector.tensor_sub(out=shift[:], in0=beta, in1=shift[:])
-            nc.vector.tensor_reduce(
-                out=offset[:], in_=tap_bias[:].rearrange("p v k i -> p v i k"), axis=mybir.AxisListType.X, op=ALU.add
-            )
-            nc.vector.tensor_add(out=offset[:], in0=offset[:], in1=shift[:])
+            nc.vector.tensor_mul(out=offset[:], in0=offset[:], in1=gain[:])
+            nc.vector.tensor_mul(out=tap_bias[:], in0=tap_bias[:], in1=gain[:].unsqueeze(2).to_broadcast(over_taps))
+            nc.vector.tensor_add(out=offset[:], in0=offset[:], in1=beta)
 
         grouped = [
             keep.tile([P, UNIT_GROUPS, CB * PACK], BF16, name="grouped%d" % unit, align_bytes=64)
@@ -153,65 +153,50 @@ def tile_timeception_pa_s_kernel(tc, x, w, b, dw, bn, out):
         y = {}
 
         def regroup(unit):
-            runs = V_CHANNELS // 4
-            nc.vector.tensor_copy(
-                out=grouped[unit][:].rearrange("p g (c f j) -> p g c j f", f=4, j=PACK)[:, :, 0:runs],
-                in_=raw[unit][:].rearrange("p g (j c f) -> p g c j f", f=4, j=PACK)[:, :, 0:runs],
-            )
-            nc.scalar.copy(
-                out=grouped[unit][:].rearrange("p g (o j) -> p g o j", j=PACK)[:, :, V_CHANNELS:CB],
-                in_=raw[unit][:].rearrange("p g (j o) -> p g o j", j=PACK)[:, :, V_CHANNELS:CB],
-            )
+            for gl in range(UNIT_GROUPS):
+                dst = grouped[unit][:, gl + 1 - 2 * (gl % 2), :].rearrange("p (c f j) -> p c j f", f=4, j=PACK)
+                src = raw[unit][:, gl, :].rearrange("p (j c f) -> p c j f", f=4, j=PACK)
+                if unit < 2 or (unit >= UNITS - 2 and gl >= UNIT_GROUPS // 2):
+                    nc.vector.tensor_copy(out=dst, in_=src)
+                else:
+                    nc.scalar.copy(out=dst, in_=src)
 
-        def quantise_and_multiply(unit):
+        def quantise(unit):
+            slot = unit // 2
+            for il in range(UNIT_GROUPS // 2):
+                i = (unit % 2) * (UNIT_GROUPS // 2) + il
+                z_col = (slot * PAIRS + i) * PAIR_COLS
+                nc.vector.quantize_mx(
+                    out=w_codes[:, z_col + CB : z_col + 3 * CB].bitcast(FP8X4),
+                    scales=w_scales[:, z_col + CB : z_col + 3 * CB],
+                    in_=grouped[unit][:, 2 * il : 2 * il + 2, :].rearrange("p g c -> p (g c)"),
+                )
+
+        def multiply(unit):
             slot = unit // 2
             v = BRANCH_ORDER[slot]
             if unit % 2 == 0:
                 y[v] = y_banks.tile([P, PAIRS, N_PASS], F32, name="y%d" % v)
-            for gl in range(UNIT_GROUPS):
-                g = (unit % 2) * UNIT_GROUPS + gl
-                col = (slot * PAIRS + g // 2) * PAIR_COLS + (g % 2) * 2 * CB
-                nc.vector.quantize_mx(
-                    out=w_codes[:, col : col + CB].bitcast(FP8X4),
-                    scales=w_scales[:, col : col + CB],
-                    in_=grouped[unit][:, gl, :],
-                )
-            for gl in range(UNIT_GROUPS):
-                g = (unit % 2) * UNIT_GROUPS + gl
-                col = (slot * PAIRS + g // 2) * PAIR_COLS + (g % 2) * CB
-                nc.tensor.matmul_mx(
-                    out=y[v][:, g // 2, :],
-                    lhsT=w_codes[:, col : col + P].bitcast(FP8X4),
-                    lhsT_scale=w_scales[:, col : col + P],
-                    rhs=x_codes[:, g * R : g * R + N_PASS].bitcast(FP8X4),
-                    rhs_scale=x_scales[:, g * R : g * R + N_PASS],
-                    start=(g % 2 == 0),
-                    stop=(g % 2 == 1),
-                )
+            for il in range(UNIT_GROUPS // 2):
+                i = (unit % 2) * (UNIT_GROUPS // 2) + il
+                z_col = (slot * PAIRS + i) * PAIR_COLS
+                for first, g, col in ((True, 2 * i + 1, z_col), (False, 2 * i, z_col + 2 * CB)):
+                    nc.tensor.matmul_mx(
+                        out=y[v][:, i, :],
+                        lhsT=w_codes[:, col : col + P].bitcast(FP8X4),
+                        lhsT_scale=w_scales[:, col : col + P],
+                        rhs=x_codes[:, g * R : g * R + N_PASS].bitcast(FP8X4),
+                        rhs_scale=x_scales[:, g * R : g * R + N_PASS],
+                        start=first,
+                        stop=not first,
+                    )
 
         z = keep.tile([P, PAIRS, NV, R], F32)
         z_max = keep.tile([P, PAIRS, NV, R_OUT], F32)
         y4_sb = keep.tile([P, PAIRS, R + PQ], F32)
         u4 = keep.tile([P, PAIRS, R], F32)
 
-        def epilogue_on_scalar(v):
-            if v == 0:
-                for i in range(PAIRS):
-                    nc.scalar.activation(
-                        out=z[:, i, v, :],
-                        in_=y[v][:, i, 0:R],
-                        func=ACT.Identity,
-                        scale=tap_gain[:, v, 1, i : i + 1],
-                        bias=offset[:, v, i : i + 1],
-                    )
-            if v == 4:
-                nc.scalar.copy(out=y4_sb[:, :, 0:R], in_=y[v][:, :, 0:R])
-                nc.scalar.copy(out=y4_sb[:, :, R : R + PQ], in_=y[v][:, :, R - PQ : R])
-
-        def taps_or_max(v):
-            if v == 4:
-                nc.vector.tensor_max(out=u4[:], in0=y4_sb[:, :, 0:R], in1=y4_sb[:, :, PQ : R + PQ])
-                return
+        def add_taps(v):
             edge = v * PQ
             for i in range(PAIRS):
                 nc.vector.tensor_scalar(
@@ -232,57 +217,52 @@ def tile_timeception_pa_s_kernel(tc, x, w, b, dw, bn, out):
                         op0=ALU.mult,
                         op1=ALU.add,
                     )
-
-        def edges_or_affine(v):
-            if v == 4:
-                for i in range(PAIRS):
-                    nc.vector.tensor_scalar(
-                        out=z[:, i, v, :],
-                        in0=u4[:, i, :],
-                        scalar1=tap_gain[:, v, 1, i : i + 1],
-                        scalar2=offset[:, v, i : i + 1],
-                        op0=ALU.mult,
-                        op1=ALU.add,
-                    )
-                return
-            edge = v * PQ
             for k, cols in ((0, slice(0, edge)), (2, slice(R - edge, R))):
-                nc.vector.tensor_sub(
+                nc.gpsimd.tensor_sub(
                     out=z[:, :, v, cols],
                     in0=z[:, :, v, cols],
                     in1=tap_bias[:, v, k, :].unsqueeze(2).to_broadcast([P, PAIRS, edge]),
                 )
 
-        def max_of_step_pairs(v):
-            steps = z[:, :, v, :].rearrange("p i (t two q) -> p i t two q", two=2, q=PQ)
+        def max_of_step_pairs(v, pairs):
+            steps = z[:, pairs, v, :].rearrange("p i (t two q) -> p i t two q", two=2, q=PQ)
             nc.vector.tensor_max(
-                out=z_max[:, :, v, :].rearrange("p i (t q) -> p i t q", q=PQ),
+                out=z_max[:, pairs, v, :].rearrange("p i (t q) -> p i t q", q=PQ),
                 in0=steps[:, :, :, 0, :],
                 in1=steps[:, :, :, 1, :],
             )
 
+        def affine_on_scalar(v, src, pairs):
+            for i in pairs:
+                nc.scalar.activation(
+                    out=z[:, i, v, :],
+                    in_=src[:, i, 0:R],
+                    func=ACT.Identity,
+                    scale=tap_gain[:, v, 1, i : i + 1],
+                    bias=offset[:, v, i : i + 1],
+                )
+
         out_rows = out.rearrange("n t p q c -> (n t p q) c")
         z_cols = z_max[:].rearrange("p i v r -> p i (v r)")
 
-        def turn_branches(first_branch):
-            turned = turn_banks.tile([P, G * CB], F32, tag="turn")
-            for i in range(PAIRS):
+        def turn_branches(turned, first_branch, pairs):
+            for i in pairs:
                 nc.tensor.transpose(
                     turned[:, i * P : (i + 1) * P],
                     z_cols[:, i, first_branch * R_OUT : first_branch * R_OUT + P],
                     ident[:],
                 )
-            return turned
 
-        def relu_shuffle_store(turned, first_branch, n_used, on_vector):
+        def relu_and_shuffle(engine, shuffled, turned, n_used, groups):
             rows = slice(0, n_used * R_OUT)
-            shuffled = keep.tile([P, CB * G], F32, name="shuffled%d" % first_branch)
-            dst = shuffled[rows, :].rearrange("p (o g) -> p o g", g=G)
-            src = turned[rows, :].rearrange("p (g o) -> p o g", o=CB)
-            if on_vector:
+            dst = shuffled[rows, :].rearrange("p (o g) -> p o g", g=G)[:, :, groups]
+            src = turned[rows, :].rearrange("p (g o) -> p o g", o=CB)[:, :, groups]
+            if engine == "vector":
                 nc.vector.tensor_scalar_max(out=dst, in0=src, scalar1=0.0)
             else:
                 nc.scalar.activation(out=dst, in_=src, func=ACT.Relu)
+
+        def store(shuffled, first_branch, n_used):
             for s in range(n_used):
                 v = first_branch + s
                 nc.sync.dma_start(
@@ -290,33 +270,59 @@ def tile_timeception_pa_s_kernel(tc, x, w, b, dw, bn, out):
                     in_=shuffled[s * R_OUT : (s + 1) * R_OUT, :],
                 )
 
+        all_pairs = slice(0, PAIRS)
         x_ps0 = turn_x(0)
         x_ps1 = turn_x(1)
         par_ps = turn_parameters()
         regroup(0)
+        regroup(1)
         copy_x(0, x_ps0)
         copy_x(1, x_ps1)
+        quantise(0)
+        quantise(1)
         unpack_parameters(par_ps)
-        regroup(1)
+        fold_without_gain()
+        regroup(2)
+        nc.scalar.activation(out=gain[:], in_=gain[:], func=ACT.Abs_reciprocal_sqrt)
         nc.vector.quantize_mx(
             out=x_codes[:, 0 : G * R].bitcast(FP8X4), scales=x_scales[:, 0 : G * R], in_=x_grouped[:]
         )
-        fold_parameters()
-        for unit in range(UNITS):
-            finished = BRANCH_ORDER[(unit - 3) // 2] if unit % 2 == 1 and unit >= 3 else None
-            if finished is not None:
-                epilogue_on_scalar(finished)
-                taps_or_max(finished)
-            quantise_and_multiply(unit)
-            if finished is not None:
-                edges_or_affine(finished)
-            if unit + 2 < UNITS:
-                regroup(unit + 2)
-            if finished is not None:
-                max_of_step_pairs(finished)
-        epilogue_on_scalar(0)
-        turned_1234 = turn_branches(1)
-        max_of_step_pairs(0)
-        relu_shuffle_store(turned_1234, 1, 4, True)
-        turned_0123 = turn_branches(0)
-        relu_shuffle_store(turned_0123, 0, 1, False)
+        fold_with_gain()
+        multiply(0)
+        multiply(1)
+        regroup(3)
+        for unit in range(2, UNITS - 2):
+            regroup(unit + 2)
+            if unit % 2 == 1:
+                add_taps(BRANCH_ORDER[(unit - 3) // 2])
+            quantise(unit)
+            multiply(unit)
+            if unit % 2 == 0 and unit >= 4:
+                max_of_step_pairs(BRANCH_ORDER[(unit - 4) // 2], all_pairs)
+
+        turned_0123 = turn_banks.tile([P, G * CB], F32, tag="turn")
+        turned_1234 = turn_banks.tile([P, G * CB], F32, tag="turn")
+        shuffled_0 = keep.tile([P, CB * G], F32)
+        shuffled_1234 = keep.tile([P, CB * G], F32)
+        nc.scalar.copy(out=y4_sb[:, :, 0:R], in_=y[4][:, :, 0:R])
+        nc.scalar.copy(out=y4_sb[:, :, R : R + PQ], in_=y[4][:, :, R - PQ : R])
+        quantise(UNITS - 2)
+        multiply(UNITS - 2)
+        affine_on_scalar(0, y[0], (0, 1))
+        max_of_step_pairs(3, all_pairs)
+        quantise(UNITS - 1)
+        multiply(UNITS - 1)
+        nc.vector.tensor_max(out=u4[:], in0=y4_sb[:, :, 0:R], in1=y4_sb[:, :, PQ : R + PQ])
+        affine_on_scalar(4, u4, (0, 1, 2, 3))
+        affine_on_scalar(0, y[0], (2, 3))
+        max_of_step_pairs(0, slice(0, 2))
+        turn_branches(turned_0123, 0, (0, 1))
+        relu_and_shuffle("scalar", shuffled_0, turned_0123, 1, slice(0, 4))
+        max_of_step_pairs(4, all_pairs)
+        turn_branches(turned_1234, 1, (0, 1, 2, 3))
+        max_of_step_pairs(0, slice(2, 4))
+        turn_branches(turned_0123, 0, (2, 3))
+        relu_and_shuffle("vector", shuffled_1234, turned_1234, 4, slice(0, G))
+        store(shuffled_1234, 1, 4)
+        relu_and_shuffle("scalar", shuffled_0, turned_0123, 1, slice(4, 8))
+        store(shuffled_0, 0, 1)

@@ -45,17 +45,16 @@ def tile_timeception_pa_s_kernel(tc, x, w, b, dw, bn, out):
         turn_banks = ctx.enter_context(tc.psum_pool(name="turn_banks", bufs=3))
         ctx.enter_context(tc.manual_schedule())
 
+        x_sb = keep.tile([P, G * K // 2], BF16)
+        nc.sync.dma_start(out=x_sb[:], in_=x.rearrange("n t p q (a c) -> (n t p q a) c", a=2))
         n_bn = NV * 4 * PAIRS
         n_b = NV * PAIRS
         n_dw = 3 * 3 * PAIRS
         par_rows = keep.tile([P, 2, P], BF16)
         nc.gpsimd.memset(par_rows[:], 0.0)
-        nc.scalar.dma_start(out=par_rows[0:n_bn, 0, :], in_=bn.rearrange("v c (i h) o -> (v c i) (h o)", h=2))
-        nc.scalar.dma_start(out=par_rows[n_bn : n_bn + n_b, 0, :], in_=b.rearrange("v (i h) o -> (v i) (h o)", h=2))
-        nc.scalar.dma_start(out=par_rows[0:n_dw, 1, :], in_=dw.rearrange("c k (i h) o -> (c k i) (h o)", h=2))
-
-        x_sb = keep.tile([P, G * K // 2], BF16)
-        nc.sync.dma_start(out=x_sb[:], in_=x.rearrange("n t p q (a c) -> (n t p q a) c", a=2))
+        nc.sync.dma_start(out=par_rows[0:n_bn, 0, :], in_=bn.rearrange("v c (i h) o -> (v c i) (h o)", h=2))
+        nc.sync.dma_start(out=par_rows[n_bn : n_bn + n_b, 0, :], in_=b.rearrange("v (i h) o -> (v i) (h o)", h=2))
+        nc.sync.dma_start(out=par_rows[0:n_dw, 1, :], in_=dw.rearrange("c k (i h) o -> (c k i) (h o)", h=2))
         raw = []
         for unit in range(UNITS):
             v = BRANCH_ORDER[unit // 2]

@@ -132,11 +132,11 @@ def tile_timeception_pa_s_kernel(tc, x, w, b, dw, bn, out):
             nc.vector.tensor_scalar_add(out=gain[:], in0=var, scalar1=EPS)
 
         def fold_without_gain():
-            nc.gpsimd.tensor_add(out=offset[:], in0=taps[:, :, 0, :], in1=taps[:, :, 1, :])
-            nc.gpsimd.tensor_mul(out=tap_bias[:], in0=taps[:], in1=bias.unsqueeze(2).to_broadcast(over_taps))
-            nc.gpsimd.tensor_add(out=offset[:], in0=offset[:], in1=taps[:, :, 2, :])
-            nc.gpsimd.tensor_mul(out=offset[:], in0=offset[:], in1=bias)
-            nc.gpsimd.tensor_sub(out=offset[:], in0=offset[:], in1=mean)
+            nc.vector.tensor_add(out=offset[:], in0=taps[:, :, 0, :], in1=taps[:, :, 1, :])
+            nc.vector.tensor_mul(out=tap_bias[:], in0=taps[:], in1=bias.unsqueeze(2).to_broadcast(over_taps))
+            nc.vector.tensor_add(out=offset[:], in0=offset[:], in1=taps[:, :, 2, :])
+            nc.vector.tensor_mul(out=offset[:], in0=offset[:], in1=bias)
+            nc.vector.tensor_sub(out=offset[:], in0=offset[:], in1=mean)
 
         def fold_with_gain():
             nc.vector.tensor_mul(out=gain[:], in0=gain[:], in1=gamma)
@@ -217,7 +217,7 @@ def tile_timeception_pa_s_kernel(tc, x, w, b, dw, bn, out):
                         op1=ALU.add,
                     )
             for k, cols in ((0, slice(0, edge)), (2, slice(R - edge, R))):
-                nc.gpsimd.tensor_sub(
+                nc.vector.tensor_sub(
                     out=z[:, :, v, cols],
                     in0=z[:, :, v, cols],
                     in1=tap_bias[:, v, k, :].unsqueeze(2).to_broadcast([P, PAIRS, edge]),

@@ -132,11 +132,11 @@ def tile_timeception_pa_s_kernel(tc, x, w, b, dw, bn, out):
             nc.vector.tensor_scalar_add(out=gain[:], in0=var, scalar1=EPS)
 
         def fold_without_gain():
-            nc.vector.tensor_add(out=offset[:], in0=taps[:, :, 0, :], in1=taps[:, :, 1, :])
-            nc.vector.tensor_mul(out=tap_bias[:], in0=taps[:], in1=bias.unsqueeze(2).to_broadcast(over_taps))
-            nc.vector.tensor_add(out=offset[:], in0=offset[:], in1=taps[:, :, 2, :])
-            nc.vector.tensor_mul(out=offset[:], in0=offset[:], in1=bias)
-            nc.vector.tensor_sub(out=offset[:], in0=offset[:], in1=mean)
+            nc.gpsimd.tensor_add(out=offset[:], in0=taps[:, :, 0, :], in1=taps[:, :, 1, :])
+            nc.gpsimd.tensor_mul(out=tap_bias[:], in0=taps[:], in1=bias.unsqueeze(2).to_broadcast(over_taps))
+            nc.gpsimd.tensor_add(out=offset[:], in0=offset[:], in1=taps[:, :, 2, :])
+            nc.gpsimd.tensor_mul(out=offset[:], in0=offset[:], in1=bias)
+            nc.gpsimd.tensor_sub(out=offset[:], in0=offset[:], in1=mean)
 
         def fold_with_gain():
             nc.vector.tensor_mul(out=gain[:], in0=gain[:], in1=gamma)
@@ -155,7 +155,7 @@ def tile_timeception_pa_s_kernel(tc, x, w, b, dw, bn, out):
             for gl in range(UNIT_GROUPS):
                 dst = grouped[unit][:, gl + 1 - 2 * (gl % 2), :].rearrange("p (c f j) -> p c j f", f=4, j=PACK)
                 src = raw[unit][:, gl, :].rearrange("p (j c f) -> p c j f", f=4, j=PACK)
-                if unit < 2 or (unit >= UNITS - 2 and gl >= UNIT_GROUPS // 2):
+                if unit < 2 or gl >= UNIT_GROUPS // 2:
                     nc.vector.tensor_copy(out=dst, in_=src)
                 else:
                     nc.scalar.copy(out=dst, in_=src)
@@ -217,7 +217,7 @@ def tile_timeception_pa_s_kernel(tc, x, w, b, dw, bn, out):
                         op1=ALU.add,
                     )
             for k, cols in ((0, slice(0, edge)), (2, slice(R - edge, R))):
-                nc.vector.tensor_sub(
+                nc.gpsimd.tensor_sub(
                     out=z[:, :, v, cols],
                     in0=z[:, :, v, cols],
                     in1=tap_bias[:, v, k, :].unsqueeze(2).to_broadcast([P, PAIRS, edge]),

@@ -155,10 +155,12 @@ def tile_timeception_pa_s_kernel(tc, x, w, b, dw, bn, out):
             for gl in range(UNIT_GROUPS):
                 dst = grouped[unit][:, gl + 1 - 2 * (gl % 2), :].rearrange("p (c f j) -> p c j f", f=4, j=PACK)
                 src = raw[unit][:, gl, :].rearrange("p (j c f) -> p c j f", f=4, j=PACK)
-                if unit < 2 or gl >= UNIT_GROUPS // 2:
+                if unit < 2:
                     nc.vector.tensor_copy(out=dst, in_=src)
-                else:
+                elif gl < UNIT_GROUPS - 1:
                     nc.scalar.copy(out=dst, in_=src)
+                else:
+                    nc.gpsimd.tensor_scalar(out=dst, in0=src, scalar1=1.0, scalar2=0.0, op0=ALU.mult, op1=ALU.add)
 
         def quantise(unit):
             slot = unit // 2

@@ -157,10 +157,8 @@ def tile_timeception_pa_s_kernel(tc, x, w, b, dw, bn, out):
                 src = raw[unit][:, gl, :].rearrange("p (j c f) -> p c j f", f=4, j=PACK)
                 if unit < 2:
                     nc.vector.tensor_copy(out=dst, in_=src)
-                elif gl < UNIT_GROUPS - 1:
-                    nc.scalar.copy(out=dst, in_=src)
                 else:
-                    nc.gpsimd.tensor_scalar(out=dst, in0=src, scalar1=1.0, scalar2=0.0, op0=ALU.mult, op1=ALU.add)
+                    nc.scalar.copy(out=dst, in_=src)
 
         def quantise(unit):
             slot = unit // 2

@@ -151,6 +151,15 @@ def tile_timeception_pa_s_kernel(tc, x, w, b, dw, bn, out):
         ]
         y = {}
 
+        def regroup_pair(unit, il, engine):
+            for gl in (2 * il, 2 * il + 1):
+                dst = grouped[unit][:, gl + 1 - 2 * (gl % 2), :].rearrange("p (c f j) -> p c j f", f=4, j=PACK)
+                src = raw[unit][:, gl, :].rearrange("p (j c f) -> p c j f", f=4, j=PACK)
+                if engine == "vector":
+                    nc.vector.tensor_copy(out=dst, in_=src)
+                else:
+                    nc.scalar.copy(out=dst, in_=src)
+
         def regroup(unit):
             for gl in range(UNIT_GROUPS):
                 dst = grouped[unit][:, gl + 1 - 2 * (gl % 2), :].rearrange("p (c f j) -> p c j f", f=4, j=PACK)
@@ -195,8 +204,7 @@ def tile_timeception_pa_s_kernel(tc, x, w, b, dw, bn, out):
         y4_sb = keep.tile([P, PAIRS, R + PQ], F32)
         u4 = keep.tile([P, PAIRS, R], F32)
 
-        def add_taps(v):
-            edge = v * PQ
+        def middle_taps(v):
             for i in range(PAIRS):
                 nc.vector.tensor_scalar(
                     out=z[:, i, v, :],
@@ -206,6 +214,9 @@ def tile_timeception_pa_s_kernel(tc, x, w, b, dw, bn, out):
                     op0=ALU.mult,
                     op1=ALU.add,
                 )
+
+        def side_taps(v):
+            edge = v * PQ
             for k, dst, src in ((0, slice(edge, R), slice(0, R - edge)), (2, slice(0, R - edge), slice(edge, R))):
                 for i in range(PAIRS):
                     nc.vector.scalar_tensor_tensor(
@@ -216,12 +227,20 @@ def tile_timeception_pa_s_kernel(tc, x, w, b, dw, bn, out):
                         op0=ALU.mult,
                         op1=ALU.add,
                     )
+
+        def mend_edges(v):
+            edge = v * PQ
             for k, cols in ((0, slice(0, edge)), (2, slice(R - edge, R))):
                 nc.gpsimd.tensor_sub(
                     out=z[:, :, v, cols],
                     in0=z[:, :, v, cols],
                     in1=tap_bias[:, v, k, :].unsqueeze(2).to_broadcast([P, PAIRS, edge]),
                 )
+
+        def add_taps(v):
+            middle_taps(v)
+            side_taps(v)
+            mend_edges(v)
 
         def max_of_step_pairs(v, pairs):
             steps = z[:, pairs, v, :].rearrange("p i (t two q) -> p i t two q", two=2, q=PQ)
@@ -244,18 +263,21 @@ def tile_timeception_pa_s_kernel(tc, x, w, b, dw, bn, out):
         out_rows = out.rearrange("n t p q c -> (n t p q) c")
         z_cols = z_max[:].rearrange("p i v r -> p i (v r)")
 
-        def turn_branches(turned, first_branch, pairs):
-            for i in pairs:
+        def turn_branches(turned, first_branch, pairs, narrow=False):
+            for n, i in enumerate(pairs):
+                col = (n if narrow else i) * P
                 nc.tensor.transpose(
-                    turned[:, i * P : (i + 1) * P],
+                    turned[:, col : col + P],
                     z_cols[:, i, first_branch * R_OUT : first_branch * R_OUT + P],
                     ident[:],
                 )
 
-        def relu_and_shuffle(engine, shuffled, turned, n_used, groups):
+        def relu_and_shuffle(engine, shuffled, turned, n_used, groups, narrow=False):
             rows = slice(0, n_used * R_OUT)
             dst = shuffled[rows, :].rearrange("p (o g) -> p o g", g=G)[:, :, groups]
-            src = turned[rows, :].rearrange("p (g o) -> p o g", o=CB)[:, :, groups]
+            src = turned[rows, :].rearrange("p (g o) -> p o g", o=CB)
+            if not narrow:
+                src = src[:, :, groups]
             if engine == "vector":
                 nc.vector.tensor_scalar_max(out=dst, in0=src, scalar1=0.0)
             else:
@@ -290,7 +312,7 @@ def tile_timeception_pa_s_kernel(tc, x, w, b, dw, bn, out):
         multiply(0)
         multiply(1)
         regroup(3)
-        for unit in range(2, UNITS - 2):
+        for unit in range(2, UNITS - 3):
             regroup(unit + 2)
             if unit % 2 == 1:
                 add_taps(BRANCH_ORDER[(unit - 3) // 2])
@@ -300,28 +322,35 @@ def tile_timeception_pa_s_kernel(tc, x, w, b, dw, bn, out):
                 max_of_step_pairs(BRANCH_ORDER[(unit - 4) // 2], all_pairs)
 
         turned_0123 = turn_banks.tile([P, G * CB], F32, tag="turn")
-        turned_1234 = turn_banks.tile([P, G * CB], F32, tag="turn")
+        turned_1234 = [turn_banks.tile([P, G * CB // 2], F32, tag="turn", name="turned_1234_%d" % n) for n in range(2)]
         shuffled_0 = keep.tile([P, CB * G], F32)
         shuffled_1234 = keep.tile([P, CB * G], F32)
+        regroup_pair(UNITS - 1, 0, "scalar")
+        quantise(UNITS - 3)
+        multiply(UNITS - 3)
+        add_taps(3)
         nc.scalar.copy(out=y4_sb[:, :, 0:R], in_=y[4][:, :, 0:R])
         nc.scalar.copy(out=y4_sb[:, :, R : R + PQ], in_=y[4][:, :, R - PQ : R])
+        regroup_pair(UNITS - 1, 1, "scalar")
         quantise(UNITS - 2)
         multiply(UNITS - 2)
-        affine_on_scalar(0, y[0], (0, 1))
-        max_of_step_pairs(3, all_pairs)
+        nc.vector.tensor_max(out=u4[:], in0=y4_sb[:, :, 0:R], in1=y4_sb[:, :, PQ : R + PQ])
         quantise(UNITS - 1)
         multiply(UNITS - 1)
-        nc.vector.tensor_max(out=u4[:], in0=y4_sb[:, :, 0:R], in1=y4_sb[:, :, PQ : R + PQ])
         affine_on_scalar(4, u4, (0, 1, 2, 3))
-        affine_on_scalar(0, y[0], (2, 3))
+        affine_on_scalar(0, y[0], (0, 1))
+        max_of_step_pairs(3, all_pairs)
+        max_of_step_pairs(4, all_pairs)
+        turn_branches(turned_1234[0], 1, (0, 1), narrow=True)
+        turn_branches(turned_1234[1], 1, (2, 3), narrow=True)
         max_of_step_pairs(0, slice(0, 2))
         turn_branches(turned_0123, 0, (0, 1))
-        relu_and_shuffle("scalar", shuffled_0, turned_0123, 1, slice(0, 4))
-        max_of_step_pairs(4, all_pairs)
-        turn_branches(turned_1234, 1, (0, 1, 2, 3))
+        affine_on_scalar(0, y[0], (2, 3))
         max_of_step_pairs(0, slice(2, 4))
         turn_branches(turned_0123, 0, (2, 3))
-        relu_and_shuffle("vector", shuffled_1234, turned_1234, 4, slice(0, G))
+        relu_and_shuffle("vector", shuffled_1234, turned_1234[0], 4, slice(0, 4), narrow=True)
+        relu_and_shuffle("scalar", shuffled_1234, turned_1234[1], 4, slice(4, 8), narrow=True)
         store(shuffled_1234, 1, 4)
+        relu_and_shuffle("vector", shuffled_0, turned_0123, 1, slice(0, 4))
         relu_and_shuffle("scalar", shuffled_0, turned_0123, 1, slice(4, 8))
         store(shuffled_0, 0, 1)

@@ -199,6 +199,17 @@ def tile_timeception_pa_s_kernel(tc, x, w, b, dw, bn, out):
                         stop=not first,
                     )
 
+        def keep_tensor_engine_busy(scratch):
+            nc.tensor.matmul_mx(
+                out=scratch[:],
+                lhsT=w_codes[:, 0:P].bitcast(FP8X4),
+                lhsT_scale=w_scales[:, 0:P],
+                rhs=x_codes[:, 0 : G * R].bitcast(FP8X4),
+                rhs_scale=x_scales[:, 0 : G * R],
+                start=True,
+                stop=True,
+            )
+
         z = keep.tile([P, PAIRS, NV, R], F32)
         z_max = keep.tile([P, PAIRS, NV, R_OUT], F32)
         y4_sb = keep.tile([P, PAIRS, R + PQ], F32)
@@ -312,12 +323,14 @@ def tile_timeception_pa_s_kernel(tc, x, w, b, dw, bn, out):
         multiply(0)
         multiply(1)
         regroup(3)
+        scratch = turn_banks.tile([P, G * R], F32, tag="turn")
         for unit in range(2, UNITS - 3):
             regroup(unit + 2)
             if unit % 2 == 1:
                 add_taps(BRANCH_ORDER[(unit - 3) // 2])
             quantise(unit)
             multiply(unit)
+            keep_tensor_engine_busy(scratch)
             if unit % 2 == 0 and unit >= 4:
                 max_of_step_pairs(BRANCH_ORDER[(unit - 4) // 2], all_pairs)
 
@@ -328,12 +341,14 @@ def tile_timeception_pa_s_kernel(tc, x, w, b, dw, bn, out):
         regroup_pair(UNITS - 1, 0, "scalar")
         quantise(UNITS - 3)
         multiply(UNITS - 3)
+        keep_tensor_engine_busy(scratch)
         add_taps(3)
         nc.scalar.copy(out=y4_sb[:, :, 0:R], in_=y[4][:, :, 0:R])
         nc.scalar.copy(out=y4_sb[:, :, R : R + PQ], in_=y[4][:, :, R - PQ : R])
         regroup_pair(UNITS - 1, 1, "scalar")
         quantise(UNITS - 2)
         multiply(UNITS - 2)
+        keep_tensor_engine_busy(scratch)
         nc.vector.tensor_max(out=u4[:], in0=y4_sb[:, :, 0:R], in1=y4_sb[:, :, PQ : R + PQ])
         quantise(UNITS - 1)
         multiply(UNITS - 1)

@@ -52,9 +52,6 @@ def tile_timeception_pa_s_kernel(tc, x, w, b, dw, bn, out):
         n_dw = 3 * 3 * PAIRS
         par_rows = keep.tile([P, 2, P], BF16)
         nc.gpsimd.memset(par_rows[:], 0.0)
-        nc.sync.dma_start(out=par_rows[0:n_bn, 0, :], in_=bn.rearrange("v c (i h) o -> (v c i) (h o)", h=2))
-        nc.sync.dma_start(out=par_rows[n_bn : n_bn + n_b, 0, :], in_=b.rearrange("v (i h) o -> (v i) (h o)", h=2))
-        nc.sync.dma_start(out=par_rows[0:n_dw, 1, :], in_=dw.rearrange("c k (i h) o -> (c k i) (h o)", h=2))
         raw = []
         for unit in range(UNITS):
             v = BRANCH_ORDER[unit // 2]
@@ -63,6 +60,10 @@ def tile_timeception_pa_s_kernel(tc, x, w, b, dw, bn, out):
             nc.sync.dma_start(
                 out=raw[unit][:], in_=w[v, g0 : g0 + UNIT_GROUPS].rearrange("g (p j) o -> p g (j o)", j=PACK)
             )
+            if unit == 1:
+                nc.sync.dma_start(out=par_rows[0:n_bn, 0, :], in_=bn.rearrange("v c (i h) o -> (v c i) (h o)", h=2))
+                nc.sync.dma_start(out=par_rows[n_bn : n_bn + n_b, 0, :], in_=b.rearrange("v (i h) o -> (v i) (h o)", h=2))
+                nc.sync.dma_start(out=par_rows[0:n_dw, 1, :], in_=dw.rearrange("c k (i h) o -> (c k i) (h o)", h=2))
 
         warm = keep.tile([P, 1], F32)
         nc.gpsimd.memset(warm[:], 1.0)

@@ -162,9 +162,9 @@ def tile_timeception_pa_s_kernel(tc, x, w, b, dw, bn, out):
                     nc.scalar.copy(out=dst, in_=src)
 
         def regroup(unit):
-            for gl in range(UNIT_GROUPS):
-                dst = grouped[unit][:, gl + 1 - 2 * (gl % 2), :].rearrange("p (c f j) -> p c j f", f=4, j=PACK)
-                src = raw[unit][:, gl, :].rearrange("p (j c f) -> p c j f", f=4, j=PACK)
+            for parity in range(2):
+                dst = grouped[unit][:, 1 - parity : UNIT_GROUPS : 2, :].rearrange("p g (c f j) -> p g c j f", f=4, j=PACK)
+                src = raw[unit][:, parity : UNIT_GROUPS : 2, :].rearrange("p g (j c f) -> p g c j f", f=4, j=PACK)
                 if unit < 2:
                     nc.vector.tensor_copy(out=dst, in_=src)
                 else:

@@ -35,6 +35,7 @@ W_COLS = NV * PAIRS * PAIR_COLS + CB
 BRANCH_ORDER = (1, 2, 3, 4, 0)
 
 FLOPS = 2 * R * K * NV * CB * G
+WARM_COLS = 480
 
 
 def tile_timeception_pa_s_kernel(tc, x, w, b, dw, bn, out):
@@ -44,6 +45,11 @@ def tile_timeception_pa_s_kernel(tc, x, w, b, dw, bn, out):
         y_banks = ctx.enter_context(tc.psum_pool(name="y_banks", bufs=1))
         turn_banks = ctx.enter_context(tc.psum_pool(name="turn_banks", bufs=3))
         ctx.enter_context(tc.manual_schedule())
+
+        zeros = keep.tile([P, WARM_COLS], F32)
+        nc.vector.memset(zeros[:], 0.0)
+        warm_ps = turn_banks.tile([P, WARM_COLS], F32, tag="turn")
+        nc.tensor.matmul(out=warm_ps[:], lhsT=zeros[:, 0:P], rhs=zeros[:], start=True, stop=True)
 
         x_sb = keep.tile([P, G * K // 2], BF16)
         nc.sync.dma_start(out=x_sb[:], in_=x.rearrange("n t p q (a c) -> (n t p q a) c", a=2))

@@ -341,7 +341,10 @@ def tile_timeception_pa_s_kernel(tc, x, w, b, dw, bn, out):
             if unit % 2 == 0 and unit >= 4:
                 max_of_step_pairs(BRANCH_ORDER[(unit - 4) // 2], all_pairs)
 
-        turned_0123 = turn_banks.tile([P, G * CB], F32, tag="turn")
+        turned_0123 = [
+            turn_banks.tile([P, G * CB // 2], F32, tag="turn", name="turned_0123_0"),
+            y_banks.tile([P, G * CB // 2], F32, name="y1"),
+        ]
         turned_1234 = [turn_banks.tile([P, G * CB // 2], F32, tag="turn", name="turned_1234_%d" % n) for n in range(2)]
         shuffled_0 = keep.tile([P, CB * G], F32)
         shuffled_1234 = keep.tile([P, CB * G], F32)
@@ -366,13 +369,13 @@ def tile_timeception_pa_s_kernel(tc, x, w, b, dw, bn, out):
         turn_branches(turned_1234[0], 1, (0, 1), narrow=True)
         turn_branches(turned_1234[1], 1, (2, 3), narrow=True)
         max_of_step_pairs(0, slice(0, 2))
-        turn_branches(turned_0123, 0, (0, 1))
+        turn_branches(turned_0123[0], 0, (0, 1), narrow=True)
         affine_on_scalar(0, y[0], (2, 3))
         max_of_step_pairs(0, slice(2, 4))
-        turn_branches(turned_0123, 0, (2, 3))
+        turn_branches(turned_0123[1], 0, (2, 3), narrow=True)
         relu_and_shuffle("vector", shuffled_1234, turned_1234[0], 4, slice(0, 4), narrow=True)
         relu_and_shuffle("scalar", shuffled_1234, turned_1234[1], 4, slice(4, 8), narrow=True)
         store(shuffled_1234, 1, 4)
-        relu_and_shuffle("vector", shuffled_0, turned_0123, 1, slice(0, 4))
-        relu_and_shuffle("scalar", shuffled_0, turned_0123, 1, slice(4, 8))
+        relu_and_shuffle("vector", shuffled_0, turned_0123[0], 1, slice(0, 4), narrow=True)
+        relu_and_shuffle("scalar", shuffled_0, turned_0123[1], 1, slice(4, 8), narrow=True)
         store(shuffled_0, 0, 1)

@@ -248,12 +248,16 @@ def tile_timeception_pa_s_kernel(tc, x, w, b, dw, bn, out):
 
         def mend_edges(v):
             edge = v * PQ
-            for k, cols in ((0, slice(0, edge)), (2, slice(R - edge, R))):
-                nc.gpsimd.tensor_sub(
-                    out=z[:, :, v, cols],
-                    in0=z[:, :, v, cols],
-                    in1=tap_bias[:, v, k, :].unsqueeze(2).to_broadcast([P, PAIRS, edge]),
-                )
+            both_ends = (
+                z[:]
+                .rearrange("p i v r -> p i (v r)")[:, :, v * R : v * R + 2 * (R - edge)]
+                .rearrange("p i (s c) -> p i s c", s=2)[:, :, :, 0:edge]
+            )
+            nc.gpsimd.tensor_sub(
+                out=both_ends,
+                in0=both_ends,
+                in1=tap_bias[:, v, 0:3:2, :].rearrange("p k i -> p i k").unsqueeze(3).to_broadcast([P, PAIRS, 2, edge]),
+            )
 
         def add_taps(v):
             middle_taps(v)
@@ -301,10 +305,10 @@ def tile_timeception_pa_s_kernel(tc, x, w, b, dw, bn, out):
             else:
                 nc.scalar.activation(out=dst, in_=src, func=ACT.Relu)
 
-        def store(shuffled, first_branch, n_used):
+        def store(queue, shuffled, first_branch, n_used):
             for s in range(n_used):
                 v = first_branch + s
-                nc.sync.dma_start(
+                queue.dma_start(
                     out=out_rows[:, v * CB * G : (v + 1) * CB * G],
                     in_=shuffled[s * R_OUT : (s + 1) * R_OUT, :],
                 )
@@ -375,7 +379,7 @@ def tile_timeception_pa_s_kernel(tc, x, w, b, dw, bn, out):
         turn_branches(turned_0123[1], 0, (2, 3), narrow=True)
         relu_and_shuffle("vector", shuffled_1234, turned_1234[0], 4, slice(0, 4), narrow=True)
         relu_and_shuffle("scalar", shuffled_1234, turned_1234[1], 4, slice(4, 8), narrow=True)
-        store(shuffled_1234, 1, 4)
+        store(nc.sync, shuffled_1234, 1, 4)
         relu_and_shuffle("vector", shuffled_0, turned_0123[0], 1, slice(0, 4), narrow=True)
         relu_and_shuffle("scalar", shuffled_0, turned_0123[1], 1, slice(4, 8), narrow=True)
-        store(shuffled_0, 0, 1)
+        store(nc.scalar, shuffled_0, 0, 1)

@@ -134,9 +134,14 @@ def tile_timeception_pa_s_kernel(tc, x, w, b, dw, bn, out):
             return par_ps
 
         def unpack_parameters(par_ps):
-            nc.vector.tensor_copy(out=par[:], in_=par_ps[:, 0, 0 : n_bn + n_b])
-            nc.vector.tensor_copy(out=taps[:, 1:4].rearrange("p c k i -> p (c k i)"), in_=par_ps[:, 1, 0:n_dw])
-            nc.vector.tensor_scalar_add(out=gain[:], in0=var, scalar1=EPS)
+            nc.scalar.copy(out=par[:], in_=par_ps[:, 0, 0 : n_bn + n_b])
+            nc.scalar.copy(out=taps[:, 1:4].rearrange("p c k i -> p (c k i)"), in_=par_ps[:, 1, 0:n_dw])
+            nc.scalar.activation(
+                out=gain[:],
+                in_=par_ps[:, 0, 0:n_bn].rearrange("p (v c i) -> p v c i", c=4, i=PAIRS)[:, :, 3, :],
+                func=ACT.Abs_reciprocal_sqrt,
+                bias=EPS,
+            )
 
         def fold_without_gain():
             nc.gpsimd.tensor_add(out=offset[:], in0=taps[:, :, 0, :], in1=taps[:, :, 1, :])
@@ -149,8 +154,8 @@ def tile_timeception_pa_s_kernel(tc, x, w, b, dw, bn, out):
             nc.vector.tensor_mul(out=gain[:], in0=gain[:], in1=gamma)
             nc.vector.tensor_mul(out=tap_gain[:], in0=taps[:], in1=gain[:].unsqueeze(2).to_broadcast(over_taps))
             nc.vector.tensor_mul(out=offset[:], in0=offset[:], in1=gain[:])
-            nc.vector.tensor_mul(out=tap_bias[:], in0=tap_bias[:], in1=gain[:].unsqueeze(2).to_broadcast(over_taps))
             nc.vector.tensor_add(out=offset[:], in0=offset[:], in1=beta)
+            nc.gpsimd.tensor_mul(out=tap_bias[:], in0=tap_bias[:], in1=gain[:].unsqueeze(2).to_broadcast(over_taps))
 
         grouped = [
             keep.tile([P, UNIT_GROUPS, CB * PACK], BF16, name="grouped%d" % unit, align_bytes=64)
@@ -272,6 +277,14 @@ def tile_timeception_pa_s_kernel(tc, x, w, b, dw, bn, out):
                 in1=steps[:, :, :, 1, :],
             )
 
+        def max_of_step_pairs_of_convolutions():
+            steps = z[:, :, 1:4, :].rearrange("p i v (t two q) -> p i v t two q", two=2, q=PQ)
+            nc.vector.tensor_max(
+                out=z_max[:, :, 1:4, :].rearrange("p i v (t q) -> p i v t q", q=PQ),
+                in0=steps[:, :, :, :, 0, :],
+                in1=steps[:, :, :, :, 1, :],
+            )
+
         def affine_on_scalar(v, src, pairs):
             for i in pairs:
                 nc.scalar.activation(
@@ -321,12 +334,11 @@ def tile_timeception_pa_s_kernel(tc, x, w, b, dw, bn, out):
         regroup(1)
         copy_x(0, x_ps0)
         copy_x(1, x_ps1)
+        unpack_parameters(par_ps)
         quantise(0)
         quantise(1)
-        unpack_parameters(par_ps)
         fold_without_gain()
         regroup(2)
-        nc.scalar.activation(out=gain[:], in_=gain[:], func=ACT.Abs_reciprocal_sqrt)
         nc.vector.quantize_mx(
             out=x_codes[:, 0 : G * R].bitcast(FP8X4), scales=x_scales[:, 0 : G * R], in_=x_grouped[:]
         )
@@ -342,8 +354,6 @@ def tile_timeception_pa_s_kernel(tc, x, w, b, dw, bn, out):
             quantise(unit)
             multiply(unit)
             keep_tensor_engine_busy(scratch)
-            if unit % 2 == 0 and unit >= 4:
-                max_of_step_pairs(BRANCH_ORDER[(unit - 4) // 2], all_pairs)
 
         turned_0123 = [
             turn_banks.tile([P, G * CB // 2], F32, tag="turn", name="turned_0123_0"),
@@ -368,7 +378,7 @@ def tile_timeception_pa_s_kernel(tc, x, w, b, dw, bn, out):
         multiply(UNITS - 1)
         affine_on_scalar(4, u4, (0, 1, 2, 3))
         affine_on_scalar(0, y[0], (0, 1))
-        max_of_step_pairs(3, all_pairs)
+        max_of_step_pairs_of_convolutions()
         max_of_step_pairs(4, all_pairs)
         turn_branches(turned_1234[0], 1, (0, 1), narrow=True)
         turn_branches(turned_1234[1], 1, (2, 3), narrow=True)

from contextlib import ExitStack

import concourse.mybir as mybir
from concourse.masks import make_identity

F32 = mybir.dt.float32
BF16 = mybir.dt.bfloat16
U32 = mybir.dt.uint32
U8 = mybir.dt.uint8
I32 = mybir.dt.int32
FP8X4 = mybir.dt.float8_e4m3fn_x4
ALU = mybir.AluOpType
ACT = mybir.ActivationFunctionType

P = 128
PACK = 4
T = 16
PQ = 4
R = T * PQ
G = 8
K = P * PACK
CB = 64
NV = 5
PAIRS = G // 2
EPS = 1e-3
R_OUT = R // 2
N_PASS = 128

UNIT_GROUPS = 4
UNITS = NV * G // UNIT_GROUPS

PAIR_COLS = 3 * CB
W_COLS = NV * PAIRS * PAIR_COLS + CB

BRANCH_ORDER = (1, 2, 3, 4, 0)

FLOPS = 2 * R * K * NV * CB * G
WARM_COLS = 480


def tile_timeception_pa_s_kernel(tc, x, w, b, dw, bn, out):
    nc = tc.nc
    with ExitStack() as ctx:
        keep = ctx.enter_context(tc.tile_pool(name="keep", bufs=1))
        y_banks = ctx.enter_context(tc.psum_pool(name="y_banks", bufs=1))
        turn_banks = ctx.enter_context(tc.psum_pool(name="turn_banks", bufs=3))
        ctx.enter_context(tc.manual_schedule())

        zeros = keep.tile([P, WARM_COLS], F32)
        nc.vector.memset(zeros[:], 0.0)
        warm_ps = turn_banks.tile([P, WARM_COLS], F32, tag="turn")
        nc.tensor.matmul(out=warm_ps[:], lhsT=zeros[:, 0:P], rhs=zeros[:], start=True, stop=True)

        x_sb = keep.tile([P, G * K // 2], BF16)
        nc.sync.dma_start(out=x_sb[:], in_=x.rearrange("n t p q (a c) -> (n t p q a) c", a=2))
        n_bn = NV * 4 * PAIRS
        n_b = NV * PAIRS
        n_dw = 3 * 3 * PAIRS
        par_rows = keep.tile([P, 2, P], BF16)
        nc.gpsimd.memset(par_rows[:], 0.0)
        raw = []
        for unit in range(UNITS):
            v = BRANCH_ORDER[unit // 2]
            g0 = (unit % 2) * UNIT_GROUPS
            raw.append(keep.tile([P, UNIT_GROUPS, PACK * CB], BF16, name="raw%d" % unit))
            nc.sync.dma_start(
                out=raw[unit][:], in_=w[v, g0 : g0 + UNIT_GROUPS].rearrange("g (p j) o -> p g (j o)", j=PACK)
            )
            if unit == 1:
                nc.sync.dma_start(out=par_rows[0:n_bn, 0, :], in_=bn.rearrange("v c (i h) o -> (v c i) (h o)", h=2))
                nc.sync.dma_start(out=par_rows[n_bn : n_bn + n_b, 0, :], in_=b.rearrange("v (i h) o -> (v i) (h o)", h=2))
                nc.sync.dma_start(out=par_rows[0:n_dw, 1, :], in_=dw.rearrange("c k (i h) o -> (c k i) (h o)", h=2))

        warm = keep.tile([P, 1], F32)
        nc.gpsimd.memset(warm[:], 1.0)
        nc.scalar.activation(out=warm[:], in_=warm[:], func=ACT.Abs_reciprocal_sqrt)
        ident = keep.tile([P, P], F32)
        make_identity(nc, ident[:])
        ident_bf = keep.tile([P, P], BF16)
        make_identity(nc, ident_bf[:])

        w_codes = keep.tile([P, W_COLS], U32, align_bytes=64)
        w_scales = keep.tile([P, W_COLS], U8, align_bytes=64)
        x_codes = keep.tile([P, G * R + R], U32, align_bytes=64)
        x_scales = keep.tile([P, G * R + R], U8, align_bytes=64)
        for plane, per_word in ((w_codes, 1), (w_scales, 4)):
            words = plane[:].bitcast(I32)
            body = (W_COLS - CB) // per_word
            nc.vector.memset(
                words[:, 0:body].rearrange("p (n c) -> p n c", c=PAIR_COLS // per_word)[:, :, 0 : CB // per_word], 0
            )
            nc.vector.memset(words[:, body:], 0)
        nc.vector.memset(x_codes[:].bitcast(I32)[:, G * R :], 0)
        nc.vector.memset(x_scales[:].bitcast(I32)[:, G * R // 4 :], 0)

        x_words = x_sb[:].bitcast(F32).rearrange("p (gh q u) -> p gh u q", gh=G // 2, u=2)
        x_grouped = keep.tile([P, G * R * PACK], BF16, align_bytes=64)
        x_grouped_words = x_grouped[:].bitcast(F32).rearrange(
            "p (a bk gl r u) -> p a bk gl r u", a=2, bk=2, gl=2, u=2
        )

        def turn_x(bk):
            x_ps = turn_banks.tile([P, 2, 2, P], F32, tag="turn")
            for gl in range(2):
                for u in range(2):
                    nc.tensor.transpose(x_ps[:, gl, u, :], x_words[:, 2 * bk + gl, u, :], ident[:])
            return x_ps

        def copy_x(bk, x_ps):
            by_half = x_ps[:].rearrange("p gl u (r a) -> p a gl r u", a=2)
            for a in range(2):
                nc.scalar.copy(out=x_grouped_words[:, a, bk], in_=by_half[:, a])

        par = keep.tile([P, n_bn + n_b], F32)
        bn_cols = par[:, 0:n_bn].rearrange("p (v c i) -> p v c i", c=4, i=PAIRS)
        gamma = bn_cols[:, :, 0, :]
        beta = bn_cols[:, :, 1, :]
        mean = bn_cols[:, :, 2, :]
        var = bn_cols[:, :, 3, :]
        bias = par[:, n_bn : n_bn + n_b].rearrange("p (v i) -> p v i", i=PAIRS)
        taps = keep.tile([P, NV, 3, PAIRS], F32)
        nc.gpsimd.memset(taps[:], 0.0)
        nc.gpsimd.memset(taps[:, 0 : NV : NV - 1, 1, :], 1.0)
        gain = keep.tile([P, NV, PAIRS], F32)
        offset = keep.tile([P, NV, PAIRS], F32)
        tap_gain = keep.tile([P, NV, 3, PAIRS], F32)
        tap_bias = keep.tile([P, NV, 3, PAIRS], F32)
        over_taps = [P, NV, 3, PAIRS]

        def turn_parameters():
            par_ps = turn_banks.tile([P, 2, P], BF16, tag="turn")
            for s in range(2):
                nc.tensor.transpose(par_ps[:, s, :], par_rows[:, s, :], ident_bf[:])
            return par_ps

        def unpack_parameters(par_ps):
            nc.scalar.copy(out=par[:], in_=par_ps[:, 0, 0 : n_bn + n_b])
            nc.scalar.copy(out=taps[:, 1:4].rearrange("p c k i -> p (c k i)"), in_=par_ps[:, 1, 0:n_dw])
            nc.scalar.activation(
                out=gain[:],
                in_=par_ps[:, 0, 0:n_bn].rearrange("p (v c i) -> p v c i", c=4, i=PAIRS)[:, :, 3, :],
                func=ACT.Abs_reciprocal_sqrt,
                bias=EPS,
            )

        def fold_without_gain():
            nc.gpsimd.tensor_add(out=offset[:], in0=taps[:, :, 0, :], in1=taps[:, :, 1, :])
            nc.gpsimd.tensor_mul(out=tap_bias[:], in0=taps[:], in1=bias.unsqueeze(2).to_broadcast(over_taps))
            nc.gpsimd.tensor_add(out=offset[:], in0=offset[:], in1=taps[:, :, 2, :])
            nc.gpsimd.tensor_mul(out=offset[:], in0=offset[:], in1=bias)
            nc.gpsimd.tensor_sub(out=offset[:], in0=offset[:], in1=mean)

        def fold_with_gain():
            nc.vector.tensor_mul(out=gain[:], in0=gain[:], in1=gamma)
            nc.vector.tensor_mul(out=tap_gain[:], in0=taps[:], in1=gain[:].unsqueeze(2).to_broadcast(over_taps))
            nc.vector.tensor_mul(out=offset[:], in0=offset[:], in1=gain[:])
            nc.vector.tensor_add(out=offset[:], in0=offset[:], in1=beta)
            nc.gpsimd.tensor_mul(out=tap_bias[:], in0=tap_bias[:], in1=gain[:].unsqueeze(2).to_broadcast(over_taps))

        grouped = [
            keep.tile([P, UNIT_GROUPS, CB * PACK], BF16, name="grouped%d" % unit, align_bytes=64)
            for unit in range(UNITS)
        ]
        y = {}

        def regroup_pair(unit, il, engine):
            for gl in (2 * il, 2 * il + 1):
                dst = grouped[unit][:, gl + 1 - 2 * (gl % 2), :].rearrange("p (c f j) -> p c j f", f=4, j=PACK)
                src = raw[unit][:, gl, :].rearrange("p (j c f) -> p c j f", f=4, j=PACK)
                if engine == "vector":
                    nc.vector.tensor_copy(out=dst, in_=src)
                else:
                    nc.scalar.copy(out=dst, in_=src)

        def regroup(unit):
            for parity in range(2):
                dst = grouped[unit][:, 1 - parity : UNIT_GROUPS : 2, :].rearrange("p g (c f j) -> p g c j f", f=4, j=PACK)
                src = raw[unit][:, parity : UNIT_GROUPS : 2, :].rearrange("p g (j c f) -> p g c j f", f=4, j=PACK)
                if unit < 2:
                    nc.vector.tensor_copy(out=dst, in_=src)
                else:
                    nc.scalar.copy(out=dst, in_=src)

        def quantise(unit):
            slot = unit // 2
            for il in range(UNIT_GROUPS // 2):
                i = (unit % 2) * (UNIT_GROUPS // 2) + il
                z_col = (slot * PAIRS + i) * PAIR_COLS
                nc.vector.quantize_mx(
                    out=w_codes[:, z_col + CB : z_col + 3 * CB].bitcast(FP8X4),
                    scales=w_scales[:, z_col + CB : z_col + 3 * CB],
                    in_=grouped[unit][:, 2 * il : 2 * il + 2, :].rearrange("p g c -> p (g c)"),
                )

        def multiply(unit):
            slot = unit // 2
            v = BRANCH_ORDER[slot]
            if unit % 2 == 0:
                y[v] = y_banks.tile([P, PAIRS, N_PASS], F32, name="y%d" % v)
            for il in range(UNIT_GROUPS // 2):
                i = (unit % 2) * (UNIT_GROUPS // 2) + il
                z_col = (slot * PAIRS + i) * PAIR_COLS
                for first, g, col in ((True, 2 * i + 1, z_col), (False, 2 * i, z_col + 2 * CB)):
                    nc.tensor.matmul_mx(
                        out=y[v][:, i, :],
                        lhsT=w_codes[:, col : col + P].bitcast(FP8X4),
                        lhsT_scale=w_scales[:, col : col + P],
                        rhs=x_codes[:, g * R : g * R + N_PASS].bitcast(FP8X4),
                        rhs_scale=x_scales[:, g * R : g * R + N_PASS],
                        start=first,
                        stop=not first,
                    )

        def keep_tensor_engine_busy(scratch):
            nc.tensor.matmul_mx(
                out=scratch[:],
                lhsT=w_codes[:, 0:P].bitcast(FP8X4),
                lhsT_scale=w_scales[:, 0:P],
                rhs=x_codes[:, 0 : G * R].bitcast(FP8X4),
                rhs_scale=x_scales[:, 0 : G * R],
                start=True,
                stop=True,
            )

        z = keep.tile([P, PAIRS, NV, R], F32)
        z_max = keep.tile([P, PAIRS, NV, R_OUT], F32)
        y4_sb = keep.tile([P, PAIRS, R + PQ], F32)
        u4 = keep.tile([P, PAIRS, R], F32)

        def middle_taps(v):
            for i in range(PAIRS):
                nc.vector.tensor_scalar(
                    out=z[:, i, v, :],
                    in0=y[v][:, i, 0:R],
                    scalar1=tap_gain[:, v, 1, i : i + 1],
                    scalar2=offset[:, v, i : i + 1],
                    op0=ALU.mult,
                    op1=ALU.add,
                )

        def side_taps(v):
            edge = v * PQ
            for k, dst, src in ((0, slice(edge, R), slice(0, R - edge)), (2, slice(0, R - edge), slice(edge, R))):
                for i in range(PAIRS):
                    nc.vector.scalar_tensor_tensor(
                        out=z[:, i, v, dst],
                        in0=y[v][:, i, src],
                        scalar=tap_gain[:, v, k, i : i + 1],
                        in1=z[:, i, v, dst],
                        op0=ALU.mult,
                        op1=ALU.add,
                    )

        def mend_edges(v):
            edge = v * PQ
            both_ends = (
                z[:]
                .rearrange("p i v r -> p i (v r)")[:, :, v * R : v * R + 2 * (R - edge)]
                .rearrange("p i (s c) -> p i s c", s=2)[:, :, :, 0:edge]
            )
            nc.gpsimd.tensor_sub(
                out=both_ends,
                in0=both_ends,
                in1=tap_bias[:, v, 0:3:2, :].rearrange("p k i -> p i k").unsqueeze(3).to_broadcast([P, PAIRS, 2, edge]),
            )

        def add_taps(v):
            middle_taps(v)
            side_taps(v)
            mend_edges(v)

        def max_of_step_pairs(v, pairs):
            steps = z[:, pairs, v, :].rearrange("p i (t two q) -> p i t two q", two=2, q=PQ)
            nc.vector.tensor_max(
                out=z_max[:, pairs, v, :].rearrange("p i (t q) -> p i t q", q=PQ),
                in0=steps[:, :, :, 0, :],
                in1=steps[:, :, :, 1, :],
            )

        def max_of_step_pairs_of_convolutions():
            steps = z[:, :, 1:4, :].rearrange("p i v (t two q) -> p i v t two q", two=2, q=PQ)
            nc.vector.tensor_max(
                out=z_max[:, :, 1:4, :].rearrange("p i v (t q) -> p i v t q", q=PQ),
                in0=steps[:, :, :, :, 0, :],
                in1=steps[:, :, :, :, 1, :],
            )

        def affine_on_scalar(v, src, pairs):
            for i in pairs:
                nc.scalar.activation(
                    out=z[:, i, v, :],
                    in_=src[:, i, 0:R],
                    func=ACT.Identity,
                    scale=tap_gain[:, v, 1, i : i + 1],
                    bias=offset[:, v, i : i + 1],
                )

        out_rows = out.rearrange("n t p q c -> (n t p q) c")
        z_cols = z_max[:].rearrange("p i v r -> p i (v r)")

        def turn_branches(turned, first_branch, pairs, narrow=False):
            for n, i in enumerate(pairs):
                col = (n if narrow else i) * P
                nc.tensor.transpose(
                    turned[:, col : col + P],
                    z_cols[:, i, first_branch * R_OUT : first_branch * R_OUT + P],
                    ident[:],
                )

        def relu_and_shuffle(engine, shuffled, turned, n_used, groups, narrow=False):
            rows = slice(0, n_used * R_OUT)
            dst = shuffled[rows, :].rearrange("p (o g) -> p o g", g=G)[:, :, groups]
            src = turned[rows, :].rearrange("p (g o) -> p o g", o=CB)
            if not narrow:
                src = src[:, :, groups]
            if engine == "vector":
                nc.vector.tensor_scalar_max(out=dst, in0=src, scalar1=0.0)
            else:
                nc.scalar.activation(out=dst, in_=src, func=ACT.Relu)

        def store(queue, shuffled, first_branch, n_used):
            for s in range(n_used):
                v = first_branch + s
                queue.dma_start(
                    out=out_rows[:, v * CB * G : (v + 1) * CB * G],
                    in_=shuffled[s * R_OUT : (s + 1) * R_OUT, :],
                )

        all_pairs = slice(0, PAIRS)
        x_ps0 = turn_x(0)
        x_ps1 = turn_x(1)
        par_ps = turn_parameters()
        regroup(0)
        regroup(1)
        copy_x(0, x_ps0)
        copy_x(1, x_ps1)
        unpack_parameters(par_ps)
        quantise(0)
        quantise(1)
        fold_without_gain()
        regroup(2)
        nc.vector.quantize_mx(
            out=x_codes[:, 0 : G * R].bitcast(FP8X4), scales=x_scales[:, 0 : G * R], in_=x_grouped[:]
        )
        fold_with_gain()
        multiply(0)
        multiply(1)
        regroup(3)
        scratch = turn_banks.tile([P, G * R], F32, tag="turn")
        for unit in range(2, UNITS - 3):
            regroup(unit + 2)
            if unit % 2 == 1:
                add_taps(BRANCH_ORDER[(unit - 3) // 2])
            quantise(unit)
            multiply(unit)
            keep_tensor_engine_busy(scratch)

        turned_0123 = [
            turn_banks.tile([P, G * CB // 2], F32, tag="turn", name="turned_0123_0"),
            y_banks.tile([P, G * CB // 2], F32, name="y1"),
        ]
        turned_1234 = [turn_banks.tile([P, G * CB // 2], F32, tag="turn", name="turned_1234_%d" % n) for n in range(2)]
        shuffled_0 = keep.tile([P, CB * G], F32)
        shuffled_1234 = keep.tile([P, CB * G], F32)
        regroup_pair(UNITS - 1, 0, "scalar")
        quantise(UNITS - 3)
        multiply(UNITS - 3)
        keep_tensor_engine_busy(scratch)
        add_taps(3)
        nc.scalar.copy(out=y4_sb[:, :, 0:R], in_=y[4][:, :, 0:R])
        nc.scalar.copy(out=y4_sb[:, :, R : R + PQ], in_=y[4][:, :, R - PQ : R])
        regroup_pair(UNITS - 1, 1, "scalar")
        quantise(UNITS - 2)
        multiply(UNITS - 2)
        keep_tensor_engine_busy(scratch)
        nc.vector.tensor_max(out=u4[:], in0=y4_sb[:, :, 0:R], in1=y4_sb[:, :, PQ : R + PQ])
        quantise(UNITS - 1)
        multiply(UNITS - 1)
        affine_on_scalar(4, u4, (0, 1, 2, 3))
        affine_on_scalar(0, y[0], (0, 1))
        max_of_step_pairs_of_convolutions()
        max_of_step_pairs(4, all_pairs)
        turn_branches(turned_1234[0], 1, (0, 1), narrow=True)
        turn_branches(turned_1234[1], 1, (2, 3), narrow=True)
        max_of_step_pairs(0, slice(0, 2))
        turn_branches(turned_0123[0], 0, (0, 1), narrow=True)
        affine_on_scalar(0, y[0], (2, 3))
        max_of_step_pairs(0, slice(2, 4))
        turn_branches(turned_0123[1], 0, (2, 3), narrow=True)
        relu_and_shuffle("vector", shuffled_1234, turned_1234[0], 4, slice(0, 4), narrow=True)
        relu_and_shuffle("scalar", shuffled_1234, turned_1234[1], 4, slice(4, 8), narrow=True)
        store(nc.sync, shuffled_1234, 1, 4)
        relu_and_shuffle("vector", shuffled_0, turned_0123[0], 1, slice(0, 4), narrow=True)
        relu_and_shuffle("scalar", shuffled_0, turned_0123[1], 1, slice(4, 8), narrow=True)
        store(nc.scalar, shuffled_0, 0, 1)
